import numpy as np
import ml_dtypes


def mxq(x, axis, fmt="e4m3"):
    dtype, down = {"e4m3": (ml_dtypes.float8_e4m3fn, 7), "e5m2": (ml_dtypes.float8_e5m2, 14)}[fmt]
    v = np.moveaxis(np.asarray(x, np.float32).astype(ml_dtypes.bfloat16).astype(np.float64), axis, -1)
    blocks = v.reshape(v.shape[:-1] + (-1, 32))
    amax = np.abs(blocks).max(-1, keepdims=True)
    byte = np.maximum(np.where(amax > 0, np.frexp(amax)[1] - 1 + 127, 0) - down, 1)
    scale = np.exp2(byte - 127.0)
    codes = (blocks / scale).astype(np.float32).astype(dtype).astype(np.float64)
    return np.moveaxis((codes * scale).reshape(v.shape), -1, axis)


WIDE = False


def mx_kscale(k):
    if not WIDE:
        return np.ones(k)
    levels = np.array([10, -10, 5, -5, 0])
    if k % 512:
        return np.exp2(np.random.permutation(np.resize(levels, k // 32))).repeat(32)
    a = np.empty((k // 512, 16))
    for p in range(k // 512):
        a[p, :8] = np.random.permutation(np.resize(levels, 8))
        for g in range(8):
            far = levels[np.abs(levels - a[p, g]) >= 10]
            a[p, g + 8] = far[np.random.randint(len(far))]
    return np.exp2(a.ravel()).repeat(32)


BF16 = ml_dtypes.bfloat16


def bf(x):
    return np.asarray(x, np.float32).astype(BF16)


def f64(x):
    return np.asarray(x).astype(np.float64)


B, T, D, H, HD, FF = 4, 1024, 1024, 4, 128, 256
EPS = 1.1920928955078125e-07
DA = H * HD


def rmsnorm(x, w):
    ms = np.mean(np.square(x), axis=-1, keepdims=True)
    return x * (1.0 / np.sqrt(ms + EPS)) * w


def silu(v):
    return v / (1.0 + np.exp(-v))


def setup_inputs():
    s = mx_kscale(DA)
    t = mx_kscale(D)
    return {
        "attn_out": bf(np.random.standard_normal((B, T, DA)) * 0.3 * s),
        "x": bf(np.random.standard_normal((B, T, D))),
        "o_w": bf(np.random.standard_normal((D, DA)) * 1.5 / np.sqrt(DA) / s[None, :]),
        "norm2_w": bf(1.0 + 0.1 * np.random.standard_normal(D)),
        "scale_gamma": bf(np.random.uniform(0.5, 1.5, D) * t),
        "scale_beta": bf(np.random.standard_normal(D) * 0.2 * t),
        "gate_w": bf(np.random.standard_normal((FF, D)) / np.sqrt(D) / t[None, :]),
        "up_w": bf(np.random.standard_normal((FF, D)) / np.sqrt(D) / t[None, :]),
    }


def reference(attn_out, x, o_w, norm2_w, scale_gamma, scale_beta, gate_w, up_w):
    x1 = f64(x) + (mxq(f64(attn_out), 2, "e4m3") @ mxq(f64(o_w), 1, "e4m3").T)
    h = rmsnorm(x1, f64(norm2_w)) * f64(scale_gamma) + f64(scale_beta)
    hq = mxq(h, 2, "e4m3")
    ff = silu(hq @ mxq(f64(gate_w), 1, "e4m3").T) * (hq @ mxq(f64(up_w), 1, "e4m3").T)
    return x1, ff

@@ -1,0 +1,342 @@
+from contextlib import ExitStack
+
+import concourse.mybir as mybir
+from concourse.masks import make_identity
+
+F32 = mybir.dt.float32
+BF16 = mybir.dt.bfloat16
+U32 = mybir.dt.uint32
+U8 = mybir.dt.uint8
+FP8X4 = mybir.dt.float8_e4m3fn_x4
+ALU = mybir.AluOpType
+ACT = mybir.ActivationFunctionType
+
+P = 128
+NTOK = 4096
+DA = 512
+D = 1024
+FF = 256
+NT = NTOK // P
+NG = NT // 4
+FLOPS = 2 * NTOK * DA * D + 2 * NTOK * D * 2 * FF
+
+LY = 6
+DS = 5
+LAG = 3
+XB = 5
+W_STEPS = (4, 5, 6, 7)
+
+
+def tile_fractalblock_pb_t_kernel(tc, attn_out, x, o_w, norm2_w, scale_gamma, scale_beta, gate_w, up_w, out_0, out_1):
+    nc = tc.nc
+    attn_f = attn_out.flatten_outer_dims()
+    x_f = x.flatten_outer_dims()
+    o0_f = out_0.flatten_outer_dims()
+    o1_f = out_1.flatten_outer_dims()
+
+    with ExitStack() as ctx:
+        const = ctx.enter_context(tc.tile_pool(name="const", bufs=1))
+        io = ctx.enter_context(tc.tile_pool(name="io", bufs=XB))
+        work = ctx.enter_context(tc.tile_pool(name="work", bufs=2))
+        small = ctx.enter_context(tc.tile_pool(name="small", bufs=8))
+        psum = ctx.enter_context(tc.psum_pool(name="psum", bufs=2))
+        ctx.enter_context(tc.manual_schedule())
+
+        ident_f = const.tile([P, P], F32, name="ident_f")
+        make_identity(nc, ident_f[:])
+        ident_b = const.tile([P, P], BF16, name="ident_b")
+        make_identity(nc, ident_b[:])
+        neg_half = const.tile([P, 1], F32, name="neg_half")
+        nc.vector.memset(neg_half[:], -0.5)
+        vec = const.tile([P, P], BF16, name="vec")
+        nc.vector.memset(vec[:], 0.0)
+        vcol = const.tile([P, 24], F32, name="vcol")
+        g32 = const.tile([P, 8], F32, name="g32")
+        ow_codes = const.tile([P, D], U32, name="ow_codes", align_bytes=64)
+        ow_scales = const.tile([P, D], U8, name="ow_scales", align_bytes=64)
+        w_codes = const.tile([P, 2, 512], U32, name="w_codes", align_bytes=64)
+        w_scales = const.tile([P, 2, 512], U8, name="w_scales", align_bytes=64)
+
+        x_sb = {}
+        at_sb = {}
+
+        def load(g):
+            a = io.tile([P, 4 * DA], BF16, name="at_sb", tag="at_sb")
+            nc.sync.dma_start(out=a[:], in_=attn_f[g * 512:(g + 1) * 512, :].rearrange("(p j) k -> p (j k)", j=4))
+            at_sb[g] = a
+            xx = io.tile([P, 4, D], BF16, name="x_sb", tag="x_sb")
+            nc.sync.dma_start(out=xx[:], in_=x_f[g * 512:(g + 1) * 512, :].rearrange("(p j) d -> p j d", j=4))
+            x_sb[g] = xx
+
+        a0 = io.tile([P, 4 * DA], BF16, name="at_sb", tag="at_sb")
+        a0_src = attn_f[0:512, :].rearrange("(p j) k -> p (j k)", j=4)
+        ow_sb = work.tile([P, 8, DA], BF16, name="ow_sb", tag="H")
+        ow_src = o_w.rearrange("(t p) k -> p t k", p=P)
+        x0 = io.tile([P, 4, D], BF16, name="x_sb", tag="x_sb")
+        x0_src = x_f[0:512, :].rearrange("(p j) d -> p j d", j=4)
+        nc.sync.dma_start(out=a0[:, 0:1024], in_=a0_src[:, 0:1024])
+        nc.sync.dma_start(out=ow_sb[:, 0:4, :], in_=ow_src[:, 0:4, :])
+        nc.sync.dma_start(out=ow_sb[:, 4:8, :], in_=ow_src[:, 4:8, :])
+        nc.sync.dma_start(out=a0[:, 1024:2048], in_=a0_src[:, 1024:2048])
+        nc.sync.dma_start(out=x0[:, 0:2, :], in_=x0_src[:, 0:2, :])
+        nc.sync.dma_start(out=x0[:, 2:4, :], in_=x0_src[:, 2:4, :])
+        at_sb[0] = a0
+        x_sb[0] = x0
+        for c in range(2):
+            nc.scalar.dma_start(out=vec[0 + 4 * c:0 + 4 * c + 4, :].rearrange("t (q i) -> t q i", i=8), in_=norm2_w[c * 512:(c + 1) * 512].rearrange("(q t i) -> t q i", t=4, i=8))
+        for c in range(2):
+            nc.scalar.dma_start(out=vec[8 + 4 * c:8 + 4 * c + 4, :].rearrange("t (q i) -> t q i", i=8), in_=scale_gamma[c * 512:(c + 1) * 512].rearrange("(q t i) -> t q i", t=4, i=8))
+        for c in range(2):
+            nc.scalar.dma_start(out=vec[16 + 4 * c:16 + 4 * c + 4, :].rearrange("t (q i) -> t q i", i=8), in_=scale_beta[c * 512:(c + 1) * 512].rearrange("(q t i) -> t q i", t=4, i=8))
+        load(1)
+        w_sb = work.tile([P, 4, D], BF16, name="w_sb", tag="H")
+        nc.sync.dma_start(out=w_sb[:, 0:2, :], in_=gate_w.rearrange("(r p) k -> p r k", p=P))
+        nc.sync.dma_start(out=w_sb[:, 2:4, :], in_=up_w.rearrange("(r p) k -> p r k", p=P))
+        for g in range(2, XB):
+            load(g)
+
+        a_codes = {}
+        a_scales = {}
+        ag_t = {}
+
+        def attn_t(q, on_vector):
+            g, pi = divmod(q, 2)
+            af = at_sb[g][:].bitcast(F32)
+            ps = psum.tile([P, 2, 2, P], F32, name="at_ps", tag="tp", bufs=3)
+            for jj in range(2):
+                for u in range(2):
+                    c0 = (2 * pi + jj) * 256
+                    nc.tensor.transpose(ps[:, jj, u, :], af[:, c0 + u:c0 + 256:2], ident_f[:])
+            ag = work.tile([P, 1024], BF16, name="ag", tag="ag", bufs=3, align_bytes=64)
+            dst = ag[:].bitcast(F32).rearrange("p (t m u) -> p t m u", t=2, u=2)
+            src = ps[:].rearrange("p t u m -> p t m u")
+            if on_vector:
+                nc.vector.tensor_copy(out=dst, in_=src)
+            else:
+                nc.scalar.copy(out=dst, in_=src)
+            ag_t[q] = ag
+
+        def attn_q(q):
+            ac = work.tile([P, 256], U32, name="ac", tag="ac", bufs=4, align_bytes=64)
+            asc = work.tile([P, 256], U8, name="asc", tag="asc", bufs=4, align_bytes=64)
+            nc.vector.quantize_mx(out=ac[:].bitcast(FP8X4), scales=asc[:], in_=ag_t[q][:])
+            a_codes[q] = ac
+            a_scales[q] = asc
+
+        x1_t = {}
+        y_t = {}
+        r_t = {}
+
+        def s1(n):
+            q, jj = divmod(n, 2)
+            g, j = divmod(n, 4)
+            pss = []
+            for hf in range(2):
+                ps = psum.tile([P, 512], F32, name="s1_ps", tag="s1", bufs=3)
+                nc.tensor.matmul_mx(
+                    out=ps[:],
+                    lhsT=a_codes[q][:, jj * P:(jj + 1) * P].bitcast(FP8X4),
+                    lhsT_scale=a_scales[q][:, jj * P:(jj + 1) * P],
+                    rhs=ow_codes[:, hf * 512:(hf + 1) * 512].bitcast(FP8X4),
+                    rhs_scale=ow_scales[:, hf * 512:(hf + 1) * 512],
+                    start=True,
+                    stop=True,
+                )
+                pss.append(ps)
+            if jj == 0:
+                x1_t[q] = work.tile([P, 2, D], F32, name="x1", tag="x1", bufs=4)
+            for hf in range(2):
+                nc.vector.tensor_tensor(
+                    out=x1_t[q][:, jj, hf * 512:(hf + 1) * 512],
+                    in0=pss[hf][:],
+                    in1=x_sb[g][:, j, hf * 512:(hf + 1) * 512],
+                    op=ALU.add,
+                )
+            if jj == 1:
+                pi = q % 2
+                nc.sync.dma_start(
+                    out=o0_f[g * 512:(g + 1) * 512, :].rearrange("(p j) d -> p j d", j=4)[:, 2 * pi:2 * pi + 2, :],
+                    in_=x1_t[q][:],
+                )
+
+        def norm(n):
+            q, jj = divmod(n, 2)
+            junk = work.tile([P, D], BF16, name="junk", tag="junk", bufs=2)
+            ss = small.tile([P, 1], F32, name="ss", tag="ss")
+            nc.scalar.activation(out=junk[:], in_=x1_t[q][:, jj, :], func=ACT.Square, accum_out=ss[:])
+            sse = small.tile([P, 1], F32, name="sse", tag="sse")
+            nc.gpsimd.tensor_scalar(out=sse[:], in0=ss[:], scalar1=1.0, scalar2=2.0 ** -13, op0=ALU.mult, op1=ALU.add)
+            r = small.tile([P, 1], F32, name="r", tag="r")
+            nc.gpsimd.tensor_tensor(out=r[:], in0=sse[:], in1=neg_half[:], op=ALU.pow)
+            r_t[n] = r
+
+        def scale_y(n):
+            q, jj = divmod(n, 2)
+            y = work.tile([P, D], F32, name="y", tag="y", bufs=10)
+            nc.vector.tensor_scalar(out=y[:].rearrange("p (t z i) -> p t z i", t=4, i=8), in0=x1_t[q][:, jj, :].rearrange("p (z t i) -> p t z i", t=4, i=8), scalar1=r_t[n][:, 0:1], scalar2=None, op0=ALU.mult)
+            y_t[n] = y
+
+        H_t = {}
+        hg_t = {}
+        h_codes = {}
+        h_scales = {}
+
+        def yt(g, c8):
+            if c8 == 0:
+                H_t[g] = work.tile([P, 8, 512], BF16, name="H", tag="H")
+            ps = psum.tile([P, 4, P], F32, name="yt_ps", tag="tp", bufs=3)
+            c, t = divmod(c8, 4)
+            k0 = (2 * t + c) * P
+            for j in range(4):
+                nc.tensor.transpose(ps[:, j, :], y_t[4 * g + j][:, k0:k0 + P], ident_f[:])
+            nc.scalar.activation(
+                out=H_t[g][:, c8, :], in_=ps[:].rearrange("p j m -> p (j m)"), func=ACT.Identity,
+                scale=g32[:, c8:c8 + 1], bias=vcol[:, 16 + c8:17 + c8],
+            )
+
+        def regroup(g, c, m0, m1):
+            if c == 0:
+                hg_t[g] = work.tile([P, 2, 2048], BF16, name="hg", tag="hg", align_bytes=64)
+            dst = hg_t[g][:, c, 4 * m0:4 * m1].rearrange("p (m t) -> p m t", t=4).rearrange("p (c i) t -> p c t i", i=4)
+            src = H_t[g][:, 4 * c:4 * c + 4, m0:m1].rearrange("p t (c i) -> p c t i", i=4)
+            nc.vector.tensor_copy(out=dst, in_=src)
+
+        def hquant(g, c, m0, m1):
+            if c == 0:
+                h_codes[g] = work.tile([P, 2, 512], U32, name="hc", tag="hc", bufs=3, align_bytes=64)
+                h_scales[g] = work.tile([P, 2, 512], U8, name="hs", tag="hs", bufs=3, align_bytes=64)
+            nc.vector.quantize_mx(
+                out=h_codes[g][:, c, m0:m1].bitcast(FP8X4), scales=h_scales[g][:, c, m0:m1], in_=hg_t[g][:, c, 4 * m0:4 * m1]
+            )
+
+        ff_t = {}
+        sg_t = {}
+        up_t = {}
+
+        def s2(q, tag, nbufs):
+            g, pi = divmod(q, 2)
+            gate_ps = psum.tile([P, 2, FF], F32, name="gate_ps", tag=tag, bufs=nbufs)
+            up_ps = psum.tile([P, 2, FF], F32, name="up_ps", tag=tag, bufs=nbufs)
+            for jj in range(2):
+                j = 2 * pi + jj
+                for c in range(2):
+                    for (ps, w0) in ((gate_ps, 0), (up_ps, FF)):
+                        nc.tensor.matmul_mx(
+                            out=ps[:, jj, :],
+                            lhsT=h_codes[g][:, c, j * P:(j + 1) * P].bitcast(FP8X4),
+                            lhsT_scale=h_scales[g][:, c, j * P:(j + 1) * P],
+                            rhs=w_codes[:, c, w0:w0 + FF].bitcast(FP8X4),
+                            rhs_scale=w_scales[:, c, w0:w0 + FF],
+                            start=(c == 0),
+                            stop=(c == 1),
+                        )
+            sg = work.tile([P, 2, FF], F32, name="sg", tag="sg", bufs=2)
+            nc.scalar.activation(out=sg[:], in_=gate_ps[:], func=ACT.Silu)
+            sg_t[q] = sg
+            up_t[q] = up_ps
+
+        def ffmul(q, store_pair):
+            g, pi = divmod(q, 2)
+            if pi == 0:
+                ff_t[g] = work.tile([P, 4, FF], F32, name="ff", tag="ff", bufs=2)
+            nc.vector.tensor_tensor(out=ff_t[g][:, 2 * pi:2 * pi + 2, :], in0=up_t[q][:], in1=sg_t[q][:], op=ALU.mult)
+            dst = o1_f[g * 512:(g + 1) * 512, :].rearrange("(p j) f -> p j f", j=4)
+            if store_pair:
+                nc.sync.dma_start(out=dst[:, 2 * pi:2 * pi + 2, :], in_=ff_t[g][:, 2 * pi:2 * pi + 2, :])
+            elif pi == 1:
+                nc.sync.dma_start(out=dst, in_=ff_t[g][:])
+
+        wg = {}
+
+        wp = work.tile([P, 4, D], BF16, name="wp", tag="wp", bufs=1)
+
+        def w_perm(r):
+            nc.gpsimd.tensor_scalar(
+                out=wp[:, r, :].rearrange("p (t z i) -> p t z i", t=4, i=8),
+                in0=w_sb[:, r, :].rearrange("p (z t i) -> p t z i", t=4, i=8),
+                scalar1=1.0, scalar2=0.0, op0=ALU.mult, op1=ALU.add,
+            )
+
+        def w_prep(c, rp):
+            if c == 0 and rp == 0:
+                wg[0] = work.tile([P, 2, 2048], BF16, name="wg", tag="hg", align_bytes=64)
+            ps = psum.tile([P, 2, 4, P], BF16, name="w_ps", tag="tp", bufs=3)
+            for rr in range(2):
+                for t in range(4):
+                    k0 = (2 * t + c) * P
+                    nc.tensor.transpose(ps[:, rr, t, :], wp[:, 2 * rp + rr, k0:k0 + P], ident_b[:])
+            dst = wg[0][:, c, rp * 1024:(rp + 1) * 1024].rearrange("p (r f t) -> p r f t", r=2, t=4)
+            nc.scalar.copy(out=dst, in_=ps[:].rearrange("p r t f -> p r f t"))
+
+        def w_quant(c):
+            nc.vector.quantize_mx(out=w_codes[:, c, :].bitcast(FP8X4), scales=w_scales[:, c, :], in_=wg[0][:, c, :])
+
+        attn_t(0, True)
+        attn_q(0)
+        owg = work.tile([P, 4 * D], BF16, name="owg", tag="hg", align_bytes=64)
+        owg_f = owg[:].bitcast(F32)
+        ow_f = ow_sb[:].rearrange("p t k -> p (t k)").bitcast(F32)
+        for b in range(4):
+            ps = psum.tile([P, 2, 2, P], F32, name="ow_ps", tag="tp", bufs=3)
+            for tt in range(2):
+                for u in range(2):
+                    c0 = (2 * b + tt) * 256
+                    nc.tensor.transpose(ps[:, tt, u, :], ow_f[:, c0 + u:c0 + 256:2], ident_f[:])
+            dst = owg_f[:, b * 512:(b + 1) * 512].rearrange("p (t m u) -> p t m u", t=2, u=2)
+            src = ps[:].rearrange("p t u m -> p t m u")
+            if b % 2 == 0:
+                nc.vector.tensor_copy(out=dst, in_=src)
+            else:
+                nc.scalar.copy(out=dst, in_=src)
+                h = b // 2
+                nc.vector.quantize_mx(
+                    out=ow_codes[:, h * 512:(h + 1) * 512].bitcast(FP8X4),
+                    scales=ow_scales[:, h * 512:(h + 1) * 512],
+                    in_=owg[:, h * 2048:(h + 1) * 2048],
+                )
+        attn_t(1, True)
+        attn_q(1)
+        vps = psum.tile([P, P], BF16, name="v_ps", tag="tp", bufs=3)
+        nc.tensor.transpose(vps[:], vec[:], ident_b[:])
+        nc.vector.tensor_copy(out=vcol[:], in_=vps[:, 0:24])
+        nc.vector.scalar_tensor_tensor(out=g32[:], in0=vcol[:, 0:8], scalar=32.0, in1=vcol[:, 8:16], op0=ALU.mult, op1=ALU.mult)
+
+        plan = []
+        for g in range(XB, NG):
+            plan.append((4 * (g - XB) + 5, 0, lambda g=g: load(g)))
+        for n in range(NT):
+            plan.append((n, 40, lambda n=n: s1(n)))
+            plan.append((n + 1, 10, lambda n=n: norm(n)))
+            plan.append((n + LAG, 20, lambda n=n: scale_y(n)))
+        for q in range(2, NT // 2):
+            plan.append((2 * q - 3, 60, lambda q=q: attn_t(q, False)))
+            plan.append((2 * q - 1, 23, lambda q=q: attn_q(q)))
+        for i in range(4):
+            plan.append((i, 45, lambda i=i: w_perm(i)))
+            plan.append((W_STEPS[i], 61, lambda i=i: w_prep(i // 2, i % 2)))
+            if i % 2 == 1:
+                plan.append((W_STEPS[i] + 1, 24, lambda i=i: w_quant(i // 2)))
+        for g in range(NG):
+            s0 = 4 * g + LY
+            last = g == NG - 1
+            for c8 in range(8):
+                plan.append((s0 + c8 // 2, 30 + 20 * (c8 % 2), lambda g=g, c8=c8: yt(g, c8)))
+            plan.append((s0 + 2, 21, lambda g=g: regroup(g, 0, 0, 512)))
+            plan.append((s0 + 3, 22, lambda g=g: hquant(g, 0, 0, 512)))
+            if not last:
+                plan.append((s0 + 4, 21, lambda g=g: regroup(g, 1, 0, 512)))
+                plan.append((s0 + 5, 22, lambda g=g: hquant(g, 1, 0, 512)))
+                for pi in range(2):
+                    plan.append((s0 + DS + 2 * pi, 70, lambda g=g, pi=pi: s2(2 * g + pi, "s2", 2)))
+                    plan.append((s0 + DS + 2 * pi + 1, 80, lambda g=g, pi=pi: ffmul(2 * g + pi, False)))
+            else:
+                plan.append((s0 + 4, 21, lambda g=g: regroup(g, 1, 0, 256)))
+                plan.append((s0 + 4, 22, lambda g=g: regroup(g, 1, 256, 512)))
+                plan.append((s0 + 4, 23, lambda g=g: hquant(g, 1, 0, 256)))
+                plan.append((s0 + 4, 24, lambda g=g: hquant(g, 1, 256, 512)))
+                plan.append((s0 + 4, 70, lambda g=g: s2(2 * g, "s2", 2)))
+                plan.append((s0 + 4, 71, lambda g=g: s2(2 * g + 1, "s1", 3)))
+                plan.append((s0 + 5, 80, lambda g=g: ffmul(2 * g, True)))
+                plan.append((s0 + 5, 81, lambda g=g: ffmul(2 * g + 1, True)))
+        for item in sorted(plan, key=lambda it: (it[0], it[1])):
+            item[2]()

@@ -16,15 +16,10 @@ NTOK = 4096
 DA = 512
 D = 1024
 FF = 256
-NT = NTOK // P
-NG = NT // 4
+NQ = NTOK // (2 * P)
+NG = NQ // 2
 FLOPS = 2 * NTOK * DA * D + 2 * NTOK * D * 2 * FF
-
-LY = 6
-DS = 5
-LAG = 3
 XB = 5
-W_STEPS = (4, 5, 6, 7)
 
 
 def tile_fractalblock_pb_t_kernel(tc, attn_out, x, o_w, norm2_w, scale_gamma, scale_beta, gate_w, up_w, out_0, out_1):
@@ -38,7 +33,7 @@ def tile_fractalblock_pb_t_kernel(tc, attn_out, x, o_w, norm2_w, scale_gamma, sc
         const = ctx.enter_context(tc.tile_pool(name="const", bufs=1))
         io = ctx.enter_context(tc.tile_pool(name="io", bufs=XB))
         work = ctx.enter_context(tc.tile_pool(name="work", bufs=2))
-        small = ctx.enter_context(tc.tile_pool(name="small", bufs=8))
+        small = ctx.enter_context(tc.tile_pool(name="small", bufs=4))
         psum = ctx.enter_context(tc.psum_pool(name="psum", bufs=2))
         ctx.enter_context(tc.manual_schedule())
 
@@ -46,12 +41,17 @@ def tile_fractalblock_pb_t_kernel(tc, attn_out, x, o_w, norm2_w, scale_gamma, sc
         make_identity(nc, ident_f[:])
         ident_b = const.tile([P, P], BF16, name="ident_b")
         make_identity(nc, ident_b[:])
-        neg_half = const.tile([P, 1], F32, name="neg_half")
+        neg_half = const.tile([P, 2], F32, name="neg_half")
         nc.vector.memset(neg_half[:], -0.5)
-        vec = const.tile([P, P], BF16, name="vec")
+        vec = const.tile([P, 512], BF16, name="vec")
         nc.vector.memset(vec[:], 0.0)
-        vcol = const.tile([P, 24], F32, name="vcol")
-        g32 = const.tile([P, 8], F32, name="g32")
+        for v, src in enumerate((norm2_w, scale_gamma, scale_beta)):
+            nc.scalar.dma_start(out=vec[2 * v:2 * v + 2, :], in_=src.rearrange("(c k) -> c k", k=512))
+        vperm = const.tile([P, 512], BF16, name="vperm")
+        warm = const.tile([P, 1], F32, name="warm")
+        nc.scalar.activation(out=warm[:], in_=neg_half[:, 0:1], func=ACT.Silu)
+        vcol = const.tile([P, 4, 6], F32, name="vcol")
+        g32 = const.tile([P, 4, 2], F32, name="g32")
         ow_codes = const.tile([P, D], U32, name="ow_codes", align_bytes=64)
         ow_scales = const.tile([P, D], U8, name="ow_scales", align_bytes=64)
         w_codes = const.tile([P, 2, 512], U32, name="w_codes", align_bytes=64)
@@ -77,61 +77,54 @@ def tile_fractalblock_pb_t_kernel(tc, attn_out, x, o_w, norm2_w, scale_gamma, sc
         nc.sync.dma_start(out=a0[:, 0:1024], in_=a0_src[:, 0:1024])
         nc.sync.dma_start(out=ow_sb[:, 0:4, :], in_=ow_src[:, 0:4, :])
         nc.sync.dma_start(out=ow_sb[:, 4:8, :], in_=ow_src[:, 4:8, :])
-        nc.sync.dma_start(out=a0[:, 1024:2048], in_=a0_src[:, 1024:2048])
         nc.sync.dma_start(out=x0[:, 0:2, :], in_=x0_src[:, 0:2, :])
+        nc.sync.dma_start(out=a0[:, 1024:2048], in_=a0_src[:, 1024:2048])
         nc.sync.dma_start(out=x0[:, 2:4, :], in_=x0_src[:, 2:4, :])
         at_sb[0] = a0
         x_sb[0] = x0
-        for c in range(2):
-            nc.scalar.dma_start(out=vec[0 + 4 * c:0 + 4 * c + 4, :].rearrange("t (q i) -> t q i", i=8), in_=norm2_w[c * 512:(c + 1) * 512].rearrange("(q t i) -> t q i", t=4, i=8))
-        for c in range(2):
-            nc.scalar.dma_start(out=vec[8 + 4 * c:8 + 4 * c + 4, :].rearrange("t (q i) -> t q i", i=8), in_=scale_gamma[c * 512:(c + 1) * 512].rearrange("(q t i) -> t q i", t=4, i=8))
-        for c in range(2):
-            nc.scalar.dma_start(out=vec[16 + 4 * c:16 + 4 * c + 4, :].rearrange("t (q i) -> t q i", i=8), in_=scale_beta[c * 512:(c + 1) * 512].rearrange("(q t i) -> t q i", t=4, i=8))
-        load(1)
-        w_sb = work.tile([P, 4, D], BF16, name="w_sb", tag="H")
+        w_sb = work.tile([P, 4, D], BF16, name="w_sb", tag="w_sb", bufs=1)
         nc.sync.dma_start(out=w_sb[:, 0:2, :], in_=gate_w.rearrange("(r p) k -> p r k", p=P))
         nc.sync.dma_start(out=w_sb[:, 2:4, :], in_=up_w.rearrange("(r p) k -> p r k", p=P))
-        for g in range(2, XB):
+        for g in range(1, XB):
             load(g)
 
+        at_ps = {}
+        ag_t = {}
         a_codes = {}
         a_scales = {}
-        ag_t = {}
 
-        def attn_t(q, on_vector):
+        def at_tr(q):
             g, pi = divmod(q, 2)
             af = at_sb[g][:].bitcast(F32)
-            ps = psum.tile([P, 2, 2, P], F32, name="at_ps", tag="tp", bufs=3)
+            ps = psum.tile([P, 2, 2, P], F32, name="at_ps", tag="at", bufs=1)
             for jj in range(2):
                 for u in range(2):
                     c0 = (2 * pi + jj) * 256
                     nc.tensor.transpose(ps[:, jj, u, :], af[:, c0 + u:c0 + 256:2], ident_f[:])
+            at_ps[q] = ps
+
+        def at_cp(q, on_vector):
             ag = work.tile([P, 1024], BF16, name="ag", tag="ag", bufs=3, align_bytes=64)
             dst = ag[:].bitcast(F32).rearrange("p (t m u) -> p t m u", t=2, u=2)
-            src = ps[:].rearrange("p t u m -> p t m u")
+            src = at_ps[q][:].rearrange("p t u m -> p t m u")
             if on_vector:
                 nc.vector.tensor_copy(out=dst, in_=src)
             else:
                 nc.scalar.copy(out=dst, in_=src)
             ag_t[q] = ag
 
-        def attn_q(q):
-            ac = work.tile([P, 256], U32, name="ac", tag="ac", bufs=4, align_bytes=64)
-            asc = work.tile([P, 256], U8, name="asc", tag="asc", bufs=4, align_bytes=64)
+        def at_q(q):
+            ac = work.tile([P, 256], U32, name="ac", tag="ac", bufs=3, align_bytes=64)
+            asc = work.tile([P, 256], U8, name="asc", tag="asc", bufs=3, align_bytes=64)
             nc.vector.quantize_mx(out=ac[:].bitcast(FP8X4), scales=asc[:], in_=ag_t[q][:])
             a_codes[q] = ac
             a_scales[q] = asc
 
+        s1_ps = {}
         x1_t = {}
-        y_t = {}
-        r_t = {}
 
-        def s1(n):
-            q, jj = divmod(n, 2)
-            g, j = divmod(n, 4)
-            pss = []
-            for hf in range(2):
+        def s1_mm(q, jj, halves=(0, 1)):
+            for hf in halves:
                 ps = psum.tile([P, 512], F32, name="s1_ps", tag="s1", bufs=3)
                 nc.tensor.matmul_mx(
                     out=ps[:],
@@ -142,201 +135,321 @@ def tile_fractalblock_pb_t_kernel(tc, attn_out, x, o_w, norm2_w, scale_gamma, sc
                     start=True,
                     stop=True,
                 )
-                pss.append(ps)
-            if jj == 0:
+                s1_ps[(q, jj, hf)] = ps
+
+        def s1_add(q, jj, halves=(0, 1)):
+            g, pi = divmod(q, 2)
+            if jj == 0 and halves[0] == 0:
                 x1_t[q] = work.tile([P, 2, D], F32, name="x1", tag="x1", bufs=4)
-            for hf in range(2):
+            for hf in halves:
                 nc.vector.tensor_tensor(
                     out=x1_t[q][:, jj, hf * 512:(hf + 1) * 512],
-                    in0=pss[hf][:],
-                    in1=x_sb[g][:, j, hf * 512:(hf + 1) * 512],
+                    in0=s1_ps[(q, jj, hf)][:],
+                    in1=x_sb[g][:, 2 * pi + jj, hf * 512:(hf + 1) * 512],
                     op=ALU.add,
                 )
-            if jj == 1:
-                pi = q % 2
+            if jj == 1 and halves[-1] == 1:
                 nc.sync.dma_start(
                     out=o0_f[g * 512:(g + 1) * 512, :].rearrange("(p j) d -> p j d", j=4)[:, 2 * pi:2 * pi + 2, :],
                     in_=x1_t[q][:],
                 )
 
-        def norm(n):
-            q, jj = divmod(n, 2)
-            junk = work.tile([P, D], BF16, name="junk", tag="junk", bufs=2)
-            ss = small.tile([P, 1], F32, name="ss", tag="ss")
-            nc.scalar.activation(out=junk[:], in_=x1_t[q][:, jj, :], func=ACT.Square, accum_out=ss[:])
-            sse = small.tile([P, 1], F32, name="sse", tag="sse")
-            nc.gpsimd.tensor_scalar(out=sse[:], in0=ss[:], scalar1=1.0, scalar2=2.0 ** -13, op0=ALU.mult, op1=ALU.add)
-            r = small.tile([P, 1], F32, name="r", tag="r")
-            nc.gpsimd.tensor_tensor(out=r[:], in0=sse[:], in1=neg_half[:], op=ALU.pow)
-            r_t[n] = r
+        ss_t = {}
+        sse_t = {}
+        y_t = {}
 
-        def scale_y(n):
-            q, jj = divmod(n, 2)
-            y = work.tile([P, D], F32, name="y", tag="y", bufs=10)
-            nc.vector.tensor_scalar(out=y[:].rearrange("p (t z i) -> p t z i", t=4, i=8), in0=x1_t[q][:, jj, :].rearrange("p (z t i) -> p t z i", t=4, i=8), scalar1=r_t[n][:, 0:1], scalar2=None, op0=ALU.mult)
-            y_t[n] = y
+        def sq(q, jj):
+            if jj == 0:
+                ss_t[q] = small.tile([P, 2], F32, name="ss", tag="ss")
+            junk = work.tile([P, D], BF16, name="junk", tag="junk", bufs=2)
+            nc.scalar.activation(out=junk[:], in_=x1_t[q][:, jj, :], func=ACT.Square, accum_out=ss_t[q][:, jj:jj + 1])
+
+        def sse(q, eng=nc.vector):
+            sse_t[q] = small.tile([P, 2], F32, name="sse", tag="sse")
+            eng.tensor_scalar(out=sse_t[q][:], in0=ss_t[q][:], scalar1=2.0 ** -13, scalar2=None, op0=ALU.add)
+
+        def scale_y(q, on_vector=()):
+            r = small.tile([P, 2], F32, name="r", tag="r")
+            nc.gpsimd.tensor_tensor(out=r[:], in0=sse_t[q][:], in1=neg_half[:], op=ALU.pow)
+            y = work.tile([P, 2, D], F32, name="y", tag="y", bufs=5)
+            for jj in range(2):
+                eng = nc.vector if jj in on_vector else nc.gpsimd
+                eng.tensor_scalar(
+                    out=y[:, jj, :].rearrange("p (t z i) -> p t z i", t=4, i=8),
+                    in0=x1_t[q][:, jj, :].rearrange("p (z t i) -> p t z i", t=4, i=8),
+                    scalar1=r[:, jj:jj + 1], scalar2=0.0, op0=ALU.mult, op1=ALU.add,
+                )
+            y_t[q] = y
 
         H_t = {}
         hg_t = {}
         h_codes = {}
         h_scales = {}
+        yt_ps = {}
 
-        def yt(g, c8):
-            if c8 == 0:
-                H_t[g] = work.tile([P, 8, 512], BF16, name="H", tag="H")
-            ps = psum.tile([P, 4, P], F32, name="yt_ps", tag="tp", bufs=3)
+        def yt_tr(g, c8, j0=0, j1=4, tag="tp", nbufs=2):
             c, t = divmod(c8, 4)
             k0 = (2 * t + c) * P
-            for j in range(4):
-                nc.tensor.transpose(ps[:, j, :], y_t[4 * g + j][:, k0:k0 + P], ident_f[:])
-            nc.scalar.activation(
-                out=H_t[g][:, c8, :], in_=ps[:].rearrange("p j m -> p (j m)"), func=ACT.Identity,
-                scale=g32[:, c8:c8 + 1], bias=vcol[:, 16 + c8:17 + c8],
-            )
+            ps = psum.tile([P, j1 - j0, P], F32, name="yt_ps", tag=tag, bufs=nbufs)
+            for j in range(j0, j1):
+                nc.tensor.transpose(ps[:, j - j0, :], y_t[2 * g + j // 2][:, j % 2, k0:k0 + P], ident_f[:])
+            yt_ps[(g, c8, j0)] = ps
+
+        def yt_aff(g, c8, j0=0, j1=4, on_vector=False):
+            if c8 == 0 and j0 == 0:
+                H_t[g] = work.tile([P, 8, 512], BF16, name="H", tag="H")
+            src = yt_ps[(g, c8, j0)][:].rearrange("p j m -> p (j m)")
+            c, t = divmod(c8, 4)
+            scale = g32[:, t, c:c + 1]
+            bias = vcol[:, t, 4 + c:5 + c]
+            dst = H_t[g][:, c8, j0 * P:j1 * P]
+            if on_vector:
+                nc.vector.tensor_scalar(
+                    out=dst, in0=src, scalar1=scale, scalar2=bias, op0=ALU.mult, op1=ALU.add,
+                )
+            else:
+                nc.scalar.activation(out=dst, in_=src, func=ACT.Identity, scale=scale, bias=bias)
 
         def regroup(g, c, m0, m1):
-            if c == 0:
+            if c == 0 and m0 == 0:
                 hg_t[g] = work.tile([P, 2, 2048], BF16, name="hg", tag="hg", align_bytes=64)
             dst = hg_t[g][:, c, 4 * m0:4 * m1].rearrange("p (m t) -> p m t", t=4).rearrange("p (c i) t -> p c t i", i=4)
             src = H_t[g][:, 4 * c:4 * c + 4, m0:m1].rearrange("p t (c i) -> p c t i", i=4)
             nc.vector.tensor_copy(out=dst, in_=src)
 
         def hquant(g, c, m0, m1):
-            if c == 0:
-                h_codes[g] = work.tile([P, 2, 512], U32, name="hc", tag="hc", bufs=3, align_bytes=64)
-                h_scales[g] = work.tile([P, 2, 512], U8, name="hs", tag="hs", bufs=3, align_bytes=64)
+            if c == 0 and m0 == 0:
+                h_codes[g] = work.tile([P, 2, 512], U32, name="hc", tag="hc", bufs=2, align_bytes=64)
+                h_scales[g] = work.tile([P, 2, 512], U8, name="hs", tag="hs", bufs=2, align_bytes=64)
             nc.vector.quantize_mx(
                 out=h_codes[g][:, c, m0:m1].bitcast(FP8X4), scales=h_scales[g][:, c, m0:m1], in_=hg_t[g][:, c, 4 * m0:4 * m1]
             )
 
-        ff_t = {}
+        gu_t = {}
         sg_t = {}
-        up_t = {}
+        ff_t = {}
 
-        def s2(q, tag, nbufs):
+        def s2_mm(q, jj, tag="s2", nbufs=2):
             g, pi = divmod(q, 2)
-            gate_ps = psum.tile([P, 2, FF], F32, name="gate_ps", tag=tag, bufs=nbufs)
-            up_ps = psum.tile([P, 2, FF], F32, name="up_ps", tag=tag, bufs=nbufs)
-            for jj in range(2):
-                j = 2 * pi + jj
-                for c in range(2):
-                    for (ps, w0) in ((gate_ps, 0), (up_ps, FF)):
-                        nc.tensor.matmul_mx(
-                            out=ps[:, jj, :],
-                            lhsT=h_codes[g][:, c, j * P:(j + 1) * P].bitcast(FP8X4),
-                            lhsT_scale=h_scales[g][:, c, j * P:(j + 1) * P],
-                            rhs=w_codes[:, c, w0:w0 + FF].bitcast(FP8X4),
-                            rhs_scale=w_scales[:, c, w0:w0 + FF],
-                            start=(c == 0),
-                            stop=(c == 1),
-                        )
-            sg = work.tile([P, 2, FF], F32, name="sg", tag="sg", bufs=2)
-            nc.scalar.activation(out=sg[:], in_=gate_ps[:], func=ACT.Silu)
-            sg_t[q] = sg
-            up_t[q] = up_ps
+            if jj == 0:
+                gu_t[q] = (
+                    psum.tile([P, 2, FF], F32, name="gate_ps", tag=tag, bufs=nbufs),
+                    psum.tile([P, 2, FF], F32, name="up_ps", tag=tag, bufs=nbufs),
+                )
+            j = 2 * pi + jj
+            for c in range(2):
+                for w in range(2):
+                    nc.tensor.matmul_mx(
+                        out=gu_t[q][w][:, jj, :],
+                        lhsT=h_codes[g][:, c, j * P:(j + 1) * P].bitcast(FP8X4),
+                        lhsT_scale=h_scales[g][:, c, j * P:(j + 1) * P],
+                        rhs=w_codes[:, c, w * FF:(w + 1) * FF].bitcast(FP8X4),
+                        rhs_scale=w_scales[:, c, w * FF:(w + 1) * FF],
+                        start=(c == 0),
+                        stop=(c == 1),
+                    )
 
-        def ffmul(q, store_pair):
+        def silu(q):
+            sg = work.tile([P, 2, FF], F32, name="sg", tag="sg", bufs=2)
+            nc.scalar.activation(out=sg[:], in_=gu_t[q][0][:], func=ACT.Silu)
+            sg_t[q] = sg
+
+        def ffmul(q, store_pair=False):
             g, pi = divmod(q, 2)
             if pi == 0:
                 ff_t[g] = work.tile([P, 4, FF], F32, name="ff", tag="ff", bufs=2)
-            nc.vector.tensor_tensor(out=ff_t[g][:, 2 * pi:2 * pi + 2, :], in0=up_t[q][:], in1=sg_t[q][:], op=ALU.mult)
+            nc.vector.tensor_tensor(out=ff_t[g][:, 2 * pi:2 * pi + 2, :], in0=gu_t[q][1][:], in1=sg_t[q][:], op=ALU.mult)
             dst = o1_f[g * 512:(g + 1) * 512, :].rearrange("(p j) f -> p j f", j=4)
             if store_pair:
                 nc.sync.dma_start(out=dst[:, 2 * pi:2 * pi + 2, :], in_=ff_t[g][:, 2 * pi:2 * pi + 2, :])
             elif pi == 1:
                 nc.sync.dma_start(out=dst, in_=ff_t[g][:])
 
-        wg = {}
-
         wp = work.tile([P, 4, D], BF16, name="wp", tag="wp", bufs=1)
+        wg = work.tile([P, 2, 2048], BF16, name="wg", tag="hg", align_bytes=64)
+        w_ps = {}
 
         def w_perm(r):
-            nc.gpsimd.tensor_scalar(
+            nc.vector.tensor_copy(
                 out=wp[:, r, :].rearrange("p (t z i) -> p t z i", t=4, i=8),
-                in0=w_sb[:, r, :].rearrange("p (z t i) -> p t z i", t=4, i=8),
-                scalar1=1.0, scalar2=0.0, op0=ALU.mult, op1=ALU.add,
+                in_=w_sb[:, r, :].rearrange("p (z t i) -> p t z i", t=4, i=8),
             )
 
-        def w_prep(c, rp):
-            if c == 0 and rp == 0:
-                wg[0] = work.tile([P, 2, 2048], BF16, name="wg", tag="hg", align_bytes=64)
-            ps = psum.tile([P, 2, 4, P], BF16, name="w_ps", tag="tp", bufs=3)
+        def w_tr(c, rp):
+            ps = psum.tile([P, 2, 4, P], BF16, name="w_ps", tag="tp", bufs=2)
             for rr in range(2):
                 for t in range(4):
                     k0 = (2 * t + c) * P
                     nc.tensor.transpose(ps[:, rr, t, :], wp[:, 2 * rp + rr, k0:k0 + P], ident_b[:])
-            dst = wg[0][:, c, rp * 1024:(rp + 1) * 1024].rearrange("p (r f t) -> p r f t", r=2, t=4)
+            dst = wg[:, c, rp * 1024:(rp + 1) * 1024].rearrange("p (r f t) -> p r f t", r=2, t=4)
             nc.scalar.copy(out=dst, in_=ps[:].rearrange("p r t f -> p r f t"))
 
         def w_quant(c):
-            nc.vector.quantize_mx(out=w_codes[:, c, :].bitcast(FP8X4), scales=w_scales[:, c, :], in_=wg[0][:, c, :])
+            nc.vector.quantize_mx(out=w_codes[:, c, :].bitcast(FP8X4), scales=w_scales[:, c, :], in_=wg[:, c, :])
 
-        attn_t(0, True)
-        attn_q(0)
+        at_tr(0)
+        at_cp(0, True)
         owg = work.tile([P, 4 * D], BF16, name="owg", tag="hg", align_bytes=64)
         owg_f = owg[:].bitcast(F32)
         ow_f = ow_sb[:].rearrange("p t k -> p (t k)").bitcast(F32)
-        for b in range(4):
-            ps = psum.tile([P, 2, 2, P], F32, name="ow_ps", tag="tp", bufs=3)
+
+        def ow_prep(b, on_vector):
+            ps = psum.tile([P, 2, 2, P], F32, name="ow_ps", tag="tp", bufs=2)
             for tt in range(2):
                 for u in range(2):
                     c0 = (2 * b + tt) * 256
                     nc.tensor.transpose(ps[:, tt, u, :], ow_f[:, c0 + u:c0 + 256:2], ident_f[:])
             dst = owg_f[:, b * 512:(b + 1) * 512].rearrange("p (t m u) -> p t m u", t=2, u=2)
             src = ps[:].rearrange("p t u m -> p t m u")
-            if b % 2 == 0:
+            if on_vector:
                 nc.vector.tensor_copy(out=dst, in_=src)
             else:
                 nc.scalar.copy(out=dst, in_=src)
-                h = b // 2
-                nc.vector.quantize_mx(
-                    out=ow_codes[:, h * 512:(h + 1) * 512].bitcast(FP8X4),
-                    scales=ow_scales[:, h * 512:(h + 1) * 512],
-                    in_=owg[:, h * 2048:(h + 1) * 2048],
-                )
-        attn_t(1, True)
-        attn_q(1)
-        vps = psum.tile([P, P], BF16, name="v_ps", tag="tp", bufs=3)
-        nc.tensor.transpose(vps[:], vec[:], ident_b[:])
-        nc.vector.tensor_copy(out=vcol[:], in_=vps[:, 0:24])
-        nc.vector.scalar_tensor_tensor(out=g32[:], in0=vcol[:, 0:8], scalar=32.0, in1=vcol[:, 8:16], op0=ALU.mult, op1=ALU.mult)
+
+        def ow_quant(h):
+            nc.vector.quantize_mx(
+                out=ow_codes[:, h * 512:(h + 1) * 512].bitcast(FP8X4),
+                scales=ow_scales[:, h * 512:(h + 1) * 512],
+                in_=owg[:, h * 2048:(h + 1) * 2048],
+            )
+
+        ow_prep(0, True)
+        ow_prep(1, False)
+        at_q(0)
+        ow_prep(2, False)
+        ow_quant(0)
+        ow_prep(3, True)
+        s1_mm(0, 0, (0,))
+        s1_mm(0, 1, (0,))
+        ow_quant(1)
+        s1_add(0, 0, (0,))
+        s1_add(0, 1, (0,))
+        s1_mm(0, 0, (1,))
+        s1_mm(0, 1, (1,))
+        s1_add(0, 0, (1,))
+        s1_add(0, 1, (1,))
+        at_tr(1)
+        at_cp(1, False)
+        nc.vector.tensor_copy(out=vperm[:].rearrange("p (t q i) -> p t q i", t=4, i=8), in_=vec[:].rearrange("p (q t i) -> p t q i", t=4, i=8))
+        for r in range(4):
+            w_perm(r)
+        vps = psum.tile([P, 4, P], BF16, name="v_ps", tag="tp", bufs=2)
+        for t in range(4):
+            nc.tensor.transpose(vps[:, t, :], vperm[:, t * P:(t + 1) * P], ident_b[:])
+        nc.vector.tensor_copy(out=vcol[:], in_=vps[:, :, 0:6])
+        nc.vector.scalar_tensor_tensor(out=g32[:], in0=vcol[:, :, 0:2], scalar=32.0, in1=vcol[:, :, 2:4], op0=ALU.mult, op1=ALU.mult)
 
         plan = []
+
+        def add(step, slot, fn, *args):
+            plan.append((step, slot, lambda: fn(*args)))
+
+        FILL = 3
         for g in range(XB, NG):
-            plan.append((4 * (g - XB) + 5, 0, lambda g=g: load(g)))
-        for n in range(NT):
-            plan.append((n, 40, lambda n=n: s1(n)))
-            plan.append((n + 1, 10, lambda n=n: norm(n)))
-            plan.append((n + LAG, 20, lambda n=n: scale_y(n)))
-        for q in range(2, NT // 2):
-            plan.append((2 * q - 3, 60, lambda q=q: attn_t(q, False)))
-            plan.append((2 * q - 1, 23, lambda q=q: attn_q(q)))
-        for i in range(4):
-            plan.append((i, 45, lambda i=i: w_perm(i)))
-            plan.append((W_STEPS[i], 61, lambda i=i: w_prep(i // 2, i % 2)))
-            if i % 2 == 1:
-                plan.append((W_STEPS[i] + 1, 24, lambda i=i: w_quant(i // 2)))
-        for g in range(NG):
-            s0 = 4 * g + LY
-            last = g == NG - 1
+            add(2 * (g - XB) + 3, 0, load, g)
+        for q in range(NQ):
+            if q >= 1:
+                add(q - 1, 50 if q <= FILL else 11, at_q, q)
+            if q >= 2:
+                add(q - 2, 31, at_tr, q)
+                add(q - 2, 62, at_cp, q, q - 2 >= FILL)
+            if q >= 1:
+                add(q, 30, s1_mm, q, 0)
+                add(q, 40, s1_mm, q, 1)
+                add(q, 35, s1_add, q, 0)
+                add(q, 45, s1_add, q, 1)
+            add(q, 55, sq, q, 0)
+            if q < NQ - 1:
+                add(q + 1, 4, sq, q, 1)
+                if q < FILL:
+                    add(q + 1, 5, sse, q, nc.gpsimd)
+                else:
+                    add(q + 1, 14, sse, q)
+                add(q + 1, 15, scale_y, q)
+        for g in range(NG - 1):
+            a = 2 * g + 3
             for c8 in range(8):
-                plan.append((s0 + c8 // 2, 30 + 20 * (c8 % 2), lambda g=g, c8=c8: yt(g, c8)))
-            plan.append((s0 + 2, 21, lambda g=g: regroup(g, 0, 0, 512)))
-            plan.append((s0 + 3, 22, lambda g=g: hquant(g, 0, 0, 512)))
-            if not last:
-                plan.append((s0 + 4, 21, lambda g=g: regroup(g, 1, 0, 512)))
-                plan.append((s0 + 5, 22, lambda g=g: hquant(g, 1, 0, 512)))
-                for pi in range(2):
-                    plan.append((s0 + DS + 2 * pi, 70, lambda g=g, pi=pi: s2(2 * g + pi, "s2", 2)))
-                    plan.append((s0 + DS + 2 * pi + 1, 80, lambda g=g, pi=pi: ffmul(2 * g + pi, False)))
-            else:
-                plan.append((s0 + 4, 21, lambda g=g: regroup(g, 1, 0, 256)))
-                plan.append((s0 + 4, 22, lambda g=g: regroup(g, 1, 256, 512)))
-                plan.append((s0 + 4, 23, lambda g=g: hquant(g, 1, 0, 256)))
-                plan.append((s0 + 4, 24, lambda g=g: hquant(g, 1, 256, 512)))
-                plan.append((s0 + 4, 70, lambda g=g: s2(2 * g, "s2", 2)))
-                plan.append((s0 + 4, 71, lambda g=g: s2(2 * g + 1, "s1", 3)))
-                plan.append((s0 + 5, 80, lambda g=g: ffmul(2 * g, True)))
-                plan.append((s0 + 5, 81, lambda g=g: ffmul(2 * g + 1, True)))
+                s = a + c8 // 4
+                if s < NQ:
+                    add(s, (32, 34, 42, 43)[c8 % 4], yt_tr, g, c8)
+                    add(s, (35, 37, 46, 47)[c8 % 4], yt_aff, g, c8)
+            for c in range(2):
+                if a + 1 + c < NQ:
+                    add(a + 1 + c, 10, regroup, g, c, 0, 512)
+                    add(a + 1 + c, 12, hquant, g, c, 0, 512)
+            for pi in range(2):
+                if a + 2 + pi < NQ:
+                    add(a + 2 + pi, 61, s2_mm, 2 * g + pi, 0)
+                if a + 3 + pi < NQ:
+                    add(a + 3 + pi, 33, s2_mm, 2 * g + pi, 1)
+                    add(a + 3 + pi, 36, silu, 2 * g + pi)
+                    add(a + 3 + pi, 44, ffmul, 2 * g + pi)
+        for i in range(4):
+            add(i // 2, 60 + i % 2, w_tr, i // 2, i % 2)
+            if i % 2 == 1:
+                add(1 + i // 2, 53, w_quant, i // 2)
         for item in sorted(plan, key=lambda it: (it[0], it[1])):
             item[2]()
+
+        g = NG - 1
+        q = NQ - 1
+        for c8 in range(4, 8):
+            yt_tr(g - 1, c8, tag="s1", nbufs=3)
+        sq(q, 1)
+        regroup(g - 1, 0, 0, 512)
+        hquant(g - 1, 0, 0, 512)
+        s2_mm(q - 5, 1)
+        s2_mm(q - 4, 0)
+        yt_aff(g - 1, 4, on_vector=True)
+        silu(q - 5)
+        yt_aff(g - 1, 5)
+        sse(q)
+        yt_aff(g - 1, 6)
+        ffmul(q - 5)
+        yt_aff(g - 1, 7)
+        scale_y(q, (0,))
+        s2_mm(q - 4, 1)
+        for c8 in range(2):
+            yt_tr(g, c8, 0, 2)
+            yt_aff(g, c8, 0, 2, True)
+        for c8 in range(2, 4):
+            yt_tr(g, c8, 0, 2)
+            yt_aff(g, c8, 0, 2)
+        regroup(g - 1, 1, 0, 512)
+        silu(q - 4)
+        for c8 in range(4, 8):
+            yt_tr(g, c8, 0, 2, "s1", 3)
+        hquant(g - 1, 1, 0, 512)
+        regroup(g, 0, 0, 256)
+        for c8 in range(4, 8):
+            yt_aff(g, c8, 0, 2)
+        ffmul(q - 4)
+        hquant(g, 0, 0, 256)
+        for c8 in range(0, 4):
+            yt_tr(g, c8, 2, 4, ("tp", "s1")[c8 // 2], (2, 3)[c8 // 2])
+            yt_aff(g, c8, 2, 4, c8 % 2 == 1)
+        s2_mm(q - 3, 0)
+        s2_mm(q - 3, 1)
+        silu(q - 3)
+        regroup(g, 1, 0, 256)
+        for c8 in range(4, 8):
+            yt_tr(g, c8, 2, 4, ("tp", "s1")[c8 % 2], (2, 3)[c8 % 2])
+            yt_aff(g, c8, 2, 4, c8 % 2 == 1)
+        hquant(g, 1, 0, 256)
+        ffmul(q - 3)
+        s2_mm(q - 2, 0)
+        s2_mm(q - 2, 1)
+        silu(q - 2)
+        regroup(g, 0, 256, 512)
+        regroup(g, 1, 256, 512)
+        hquant(g, 0, 256, 512)
+        hquant(g, 1, 256, 512)
+        ffmul(q - 2)
+        s2_mm(q - 1, 0, "s1", 3)
+        s2_mm(q - 1, 1)
+        s2_mm(q, 0, "s1", 3)
+        s2_mm(q, 1)
+        silu(q - 1)
+        ffmul(q - 1, True)
+        silu(q)
+        ffmul(q, True)

@@ -20,6 +20,7 @@ NQ = NTOK // (2 * P)
 NG = NQ // 2
 FLOPS = 2 * NTOK * DA * D + 2 * NTOK * D * 2 * FF
 XB = 5
+BANKS = {"tp": 3, "s1": 3, "s2": 2}
 
 
 def tile_fractalblock_pb_t_kernel(tc, attn_out, x, o_w, norm2_w, scale_gamma, scale_beta, gate_w, up_w, out_0, out_1):
@@ -96,7 +97,7 @@ def tile_fractalblock_pb_t_kernel(tc, attn_out, x, o_w, norm2_w, scale_gamma, sc
         def at_tr(q):
             g, pi = divmod(q, 2)
             af = at_sb[g][:].bitcast(F32)
-            ps = psum.tile([P, 2, 2, P], F32, name="at_ps", tag="at", bufs=1)
+            ps = psum.tile([P, 2, 2, P], F32, name="at_ps", tag="tp", bufs=BANKS["tp"])
             for jj in range(2):
                 for u in range(2):
                     c0 = (2 * pi + jj) * 256
@@ -125,7 +126,7 @@ def tile_fractalblock_pb_t_kernel(tc, attn_out, x, o_w, norm2_w, scale_gamma, sc
 
         def s1_mm(q, jj, halves=(0, 1)):
             for hf in halves:
-                ps = psum.tile([P, 512], F32, name="s1_ps", tag="s1", bufs=3)
+                ps = psum.tile([P, 512], F32, name="s1_ps", tag="s1", bufs=BANKS["s1"])
                 nc.tensor.matmul_mx(
                     out=ps[:],
                     lhsT=a_codes[q][:, jj * P:(jj + 1) * P].bitcast(FP8X4),
@@ -187,10 +188,10 @@ def tile_fractalblock_pb_t_kernel(tc, attn_out, x, o_w, norm2_w, scale_gamma, sc
         h_scales = {}
         yt_ps = {}
 
-        def yt_tr(g, c8, j0=0, j1=4, tag="tp", nbufs=2):
+        def yt_tr(g, c8, j0=0, j1=4, tag="tp"):
             c, t = divmod(c8, 4)
             k0 = (2 * t + c) * P
-            ps = psum.tile([P, j1 - j0, P], F32, name="yt_ps", tag=tag, bufs=nbufs)
+            ps = psum.tile([P, j1 - j0, P], F32, name="yt_ps", tag=tag, bufs=BANKS[tag])
             for j in range(j0, j1):
                 nc.tensor.transpose(ps[:, j - j0, :], y_t[2 * g + j // 2][:, j % 2, k0:k0 + P], ident_f[:])
             yt_ps[(g, c8, j0)] = ps
@@ -229,41 +230,35 @@ def tile_fractalblock_pb_t_kernel(tc, attn_out, x, o_w, norm2_w, scale_gamma, sc
         sg_t = {}
         ff_t = {}
 
-        def s2_mm(q, jj, tag="s2", nbufs=2):
-            g, pi = divmod(q, 2)
-            if jj == 0:
-                gu_t[q] = (
-                    psum.tile([P, 2, FF], F32, name="gate_ps", tag=tag, bufs=nbufs),
-                    psum.tile([P, 2, FF], F32, name="up_ps", tag=tag, bufs=nbufs),
-                )
-            j = 2 * pi + jj
+        def s2_mm(n, tag="s2"):
+            g, j = divmod(n, 4)
+            gu = psum.tile([P, 2 * FF], F32, name="gu_ps", tag=tag, bufs=BANKS[tag])
             for c in range(2):
-                for w in range(2):
-                    nc.tensor.matmul_mx(
-                        out=gu_t[q][w][:, jj, :],
-                        lhsT=h_codes[g][:, c, j * P:(j + 1) * P].bitcast(FP8X4),
-                        lhsT_scale=h_scales[g][:, c, j * P:(j + 1) * P],
-                        rhs=w_codes[:, c, w * FF:(w + 1) * FF].bitcast(FP8X4),
-                        rhs_scale=w_scales[:, c, w * FF:(w + 1) * FF],
-                        start=(c == 0),
-                        stop=(c == 1),
-                    )
+                nc.tensor.matmul_mx(
+                    out=gu[:],
+                    lhsT=h_codes[g][:, c, j * P:(j + 1) * P].bitcast(FP8X4),
+                    lhsT_scale=h_scales[g][:, c, j * P:(j + 1) * P],
+                    rhs=w_codes[:, c, :].bitcast(FP8X4),
+                    rhs_scale=w_scales[:, c, :],
+                    start=(c == 0),
+                    stop=(c == 1),
+                )
+            gu_t[n] = gu
 
-        def silu(q):
-            sg = work.tile([P, 2, FF], F32, name="sg", tag="sg", bufs=2)
-            nc.scalar.activation(out=sg[:], in_=gu_t[q][0][:], func=ACT.Silu)
-            sg_t[q] = sg
+        def silu(n):
+            sg = work.tile([P, FF], F32, name="sg", tag="sg", bufs=3)
+            nc.scalar.activation(out=sg[:], in_=gu_t[n][:, 0:FF], func=ACT.Silu)
+            sg_t[n] = sg
 
-        def ffmul(q, store_pair=False):
-            g, pi = divmod(q, 2)
-            if pi == 0:
+        def ffmul(n, store_tiles=4):
+            g, j = divmod(n, 4)
+            if j == 0:
                 ff_t[g] = work.tile([P, 4, FF], F32, name="ff", tag="ff", bufs=2)
-            nc.vector.tensor_tensor(out=ff_t[g][:, 2 * pi:2 * pi + 2, :], in0=gu_t[q][1][:], in1=sg_t[q][:], op=ALU.mult)
-            dst = o1_f[g * 512:(g + 1) * 512, :].rearrange("(p j) f -> p j f", j=4)
-            if store_pair:
-                nc.sync.dma_start(out=dst[:, 2 * pi:2 * pi + 2, :], in_=ff_t[g][:, 2 * pi:2 * pi + 2, :])
-            elif pi == 1:
-                nc.sync.dma_start(out=dst, in_=ff_t[g][:])
+            nc.vector.tensor_tensor(out=ff_t[g][:, j, :], in0=gu_t[n][:, FF:2 * FF], in1=sg_t[n][:], op=ALU.mult)
+            if j % store_tiles == store_tiles - 1:
+                dst = o1_f[g * 512:(g + 1) * 512, :].rearrange("(p j) f -> p j f", j=4)
+                j0 = j + 1 - store_tiles
+                nc.sync.dma_start(out=dst[:, j0:j + 1, :], in_=ff_t[g][:, j0:j + 1, :])
 
         wp = work.tile([P, 4, D], BF16, name="wp", tag="wp", bufs=1)
         wg = work.tile([P, 2, 2048], BF16, name="wg", tag="hg", align_bytes=64)
@@ -276,7 +271,7 @@ def tile_fractalblock_pb_t_kernel(tc, attn_out, x, o_w, norm2_w, scale_gamma, sc
             )
 
         def w_tr(c, rp):
-            ps = psum.tile([P, 2, 4, P], BF16, name="w_ps", tag="tp", bufs=2)
+            ps = psum.tile([P, 2, 4, P], BF16, name="w_ps", tag="tp", bufs=BANKS["tp"])
             for rr in range(2):
                 for t in range(4):
                     k0 = (2 * t + c) * P
@@ -294,7 +289,7 @@ def tile_fractalblock_pb_t_kernel(tc, attn_out, x, o_w, norm2_w, scale_gamma, sc
         ow_f = ow_sb[:].rearrange("p t k -> p (t k)").bitcast(F32)
 
         def ow_prep(b, on_vector):
-            ps = psum.tile([P, 2, 2, P], F32, name="ow_ps", tag="tp", bufs=2)
+            ps = psum.tile([P, 2, 2, P], F32, name="ow_ps", tag="tp", bufs=BANKS["tp"])
             for tt in range(2):
                 for u in range(2):
                     c0 = (2 * b + tt) * 256
@@ -333,7 +328,7 @@ def tile_fractalblock_pb_t_kernel(tc, attn_out, x, o_w, norm2_w, scale_gamma, sc
         nc.vector.tensor_copy(out=vperm[:].rearrange("p (t q i) -> p t q i", t=4, i=8), in_=vec[:].rearrange("p (q t i) -> p t q i", t=4, i=8))
         for r in range(4):
             w_perm(r)
-        vps = psum.tile([P, 4, P], BF16, name="v_ps", tag="tp", bufs=2)
+        vps = psum.tile([P, 4, P], BF16, name="v_ps", tag="tp", bufs=BANKS["tp"])
         for t in range(4):
             nc.tensor.transpose(vps[:, t, :], vperm[:, t * P:(t + 1) * P], ident_b[:])
         nc.vector.tensor_copy(out=vcol[:], in_=vps[:, :, 0:6])
@@ -351,8 +346,11 @@ def tile_fractalblock_pb_t_kernel(tc, attn_out, x, o_w, norm2_w, scale_gamma, sc
             if q >= 1:
                 add(q - 1, 50 if q <= FILL else 11, at_q, q)
             if q >= 2:
-                add(q - 2, 31, at_tr, q)
-                add(q - 2, 62, at_cp, q, q - 2 >= FILL)
+                add(q - 2, 49, at_tr, q)
+                if q - 2 >= FILL:
+                    add(q - 1, 9.2, at_cp, q, True)
+                else:
+                    add(q - 2, 62, at_cp, q, False)
             if q >= 1:
                 add(q, 30, s1_mm, q, 0)
                 add(q, 40, s1_mm, q, 1)
@@ -371,19 +369,20 @@ def tile_fractalblock_pb_t_kernel(tc, attn_out, x, o_w, norm2_w, scale_gamma, sc
             for c8 in range(8):
                 s = a + c8 // 4
                 if s < NQ:
-                    add(s, (32, 34, 42, 43)[c8 % 4], yt_tr, g, c8)
-                    add(s, (35, 37, 46, 47)[c8 % 4], yt_aff, g, c8)
+                    add(s, (31, 32, 33, 34)[c8 % 4], yt_tr, g, c8)
+                    add(s, (34.1, 35, 36, 37)[c8 % 4], yt_aff, g, c8)
             for c in range(2):
                 if a + 1 + c < NQ:
                     add(a + 1 + c, 10, regroup, g, c, 0, 512)
                     add(a + 1 + c, 12, hquant, g, c, 0, 512)
-            for pi in range(2):
-                if a + 2 + pi < NQ:
-                    add(a + 2 + pi, 61, s2_mm, 2 * g + pi, 0)
-                if a + 3 + pi < NQ:
-                    add(a + 3 + pi, 33, s2_mm, 2 * g + pi, 1)
-                    add(a + 3 + pi, 36, silu, 2 * g + pi)
-                    add(a + 3 + pi, 44, ffmul, 2 * g + pi)
+            for j in range(4):
+                s, jj = a + 2 + j // 2 + j % 2, j % 2
+                n = 4 * g + j
+                if s < NQ:
+                    add(s, (41, 29)[jj], s2_mm, n)
+                    add(s, (57, 30)[jj], silu, n)
+                if s + 1 - jj < NQ:
+                    add(s + 1 - jj, (9.5, 38)[jj], ffmul, n)
         for i in range(4):
             add(i // 2, 60 + i % 2, w_tr, i // 2, i % 2)
             if i % 2 == 1:
@@ -393,63 +392,72 @@ def tile_fractalblock_pb_t_kernel(tc, attn_out, x, o_w, norm2_w, scale_gamma, sc
 
         g = NG - 1
         q = NQ - 1
+        n = 4 * g
+        ffmul(n - 8)
+        s2_mm(n - 7)
         for c8 in range(4, 8):
-            yt_tr(g - 1, c8, tag="s1", nbufs=3)
+            yt_tr(g - 1, c8, 0, 4, ("tp", "s1")[c8 // 7])
         sq(q, 1)
         regroup(g - 1, 0, 0, 512)
+        silu(n - 7)
         hquant(g - 1, 0, 0, 512)
-        s2_mm(q - 5, 1)
-        s2_mm(q - 4, 0)
         yt_aff(g - 1, 4, on_vector=True)
-        silu(q - 5)
         yt_aff(g - 1, 5)
+        s2_mm(n - 6)
         sse(q)
+        ffmul(n - 7)
         yt_aff(g - 1, 6)
-        ffmul(q - 5)
+        silu(n - 6)
         yt_aff(g - 1, 7)
         scale_y(q, (0,))
-        s2_mm(q - 4, 1)
-        for c8 in range(2):
-            yt_tr(g, c8, 0, 2)
-            yt_aff(g, c8, 0, 2, True)
-        for c8 in range(2, 4):
-            yt_tr(g, c8, 0, 2)
-            yt_aff(g, c8, 0, 2)
+        s2_mm(n - 5)
+        for c8 in range(4):
+            yt_tr(g, c8, 0, 2, ("tp", "s1")[c8 // 3])
+            yt_aff(g, c8, 0, 2, c8 < 2)
+        ffmul(n - 6)
+        silu(n - 5)
         regroup(g - 1, 1, 0, 512)
-        silu(q - 4)
         for c8 in range(4, 8):
-            yt_tr(g, c8, 0, 2, "s1", 3)
-        hquant(g - 1, 1, 0, 512)
+            yt_tr(g, c8, 0, 2, ("s1", "tp")[c8 // 6])
         regroup(g, 0, 0, 256)
+        hquant(g - 1, 1, 0, 512)
         for c8 in range(4, 8):
             yt_aff(g, c8, 0, 2)
-        ffmul(q - 4)
+        ffmul(n - 5)
         hquant(g, 0, 0, 256)
+        s2_mm(n - 4)
+        s2_mm(n - 3)
+        silu(n - 4)
         for c8 in range(0, 4):
-            yt_tr(g, c8, 2, 4, ("tp", "s1")[c8 // 2], (2, 3)[c8 // 2])
+            yt_tr(g, c8, 2, 4, ("tp", "s1")[c8 // 2])
             yt_aff(g, c8, 2, 4, c8 % 2 == 1)
-        s2_mm(q - 3, 0)
-        s2_mm(q - 3, 1)
-        silu(q - 3)
+        silu(n - 3)
+        ffmul(n - 4)
         regroup(g, 1, 0, 256)
         for c8 in range(4, 8):
-            yt_tr(g, c8, 2, 4, ("tp", "s1")[c8 % 2], (2, 3)[c8 % 2])
+            yt_tr(g, c8, 2, 4, ("tp", "s1")[c8 // 6])
             yt_aff(g, c8, 2, 4, c8 % 2 == 1)
         hquant(g, 1, 0, 256)
-        ffmul(q - 3)
-        s2_mm(q - 2, 0)
-        s2_mm(q - 2, 1)
-        silu(q - 2)
         regroup(g, 0, 256, 512)
         regroup(g, 1, 256, 512)
+        ffmul(n - 3)
         hquant(g, 0, 256, 512)
         hquant(g, 1, 256, 512)
-        ffmul(q - 2)
-        s2_mm(q - 1, 0, "s1", 3)
-        s2_mm(q - 1, 1)
-        s2_mm(q, 0, "s1", 3)
-        s2_mm(q, 1)
-        silu(q - 1)
-        ffmul(q - 1, True)
-        silu(q)
-        ffmul(q, True)
+        s2_mm(n - 2)
+        silu(n - 2)
+        s2_mm(n - 1, "s1")
+        silu(n - 1)
+        s2_mm(n, "s1")
+        silu(n)
+        s2_mm(n + 1, "s1")
+        silu(n + 1)
+        s2_mm(n + 2)
+        silu(n + 2)
+        ffmul(n - 2)
+        ffmul(n - 1)
+        ffmul(n, 2)
+        ffmul(n + 1, 2)
+        s2_mm(n + 3)
+        silu(n + 3)
+        ffmul(n + 2, 1)
+        ffmul(n + 3, 1)

@@ -19,6 +19,7 @@ FF = 256
 NQ = NTOK // (2 * P)
 NG = NQ // 2
 FLOPS = 2 * NTOK * DA * D + 2 * NTOK * D * 2 * FF
+WARM = 6
 XB = 5
 BANKS = {"tp": 3, "s1": 3, "s2": 2}
 
@@ -51,6 +52,8 @@ def tile_fractalblock_pb_t_kernel(tc, attn_out, x, o_w, norm2_w, scale_gamma, sc
         vperm = const.tile([P, 512], BF16, name="vperm")
         warm = const.tile([P, 1], F32, name="warm")
         nc.scalar.activation(out=warm[:], in_=neg_half[:, 0:1], func=ACT.Silu)
+        zeros = const.tile([P, 512], BF16, name="zeros")
+        nc.vector.memset(zeros[:], 0.0)
         vcol = const.tile([P, 4, 6], F32, name="vcol")
         g32 = const.tile([P, 4, 2], F32, name="g32")
         ow_codes = const.tile([P, D], U32, name="ow_codes", align_bytes=64)
@@ -115,8 +118,8 @@ def tile_fractalblock_pb_t_kernel(tc, attn_out, x, o_w, norm2_w, scale_gamma, sc
             ag_t[q] = ag
 
         def at_q(q):
-            ac = work.tile([P, 256], U32, name="ac", tag="ac", bufs=3, align_bytes=64)
-            asc = work.tile([P, 256], U8, name="asc", tag="asc", bufs=3, align_bytes=64)
+            ac = work.tile([P, 256], U32, name="ac", tag="ac", bufs=4, align_bytes=64)
+            asc = work.tile([P, 256], U8, name="asc", tag="asc", bufs=4, align_bytes=64)
             nc.vector.quantize_mx(out=ac[:].bitcast(FP8X4), scales=asc[:], in_=ag_t[q][:])
             a_codes[q] = ac
             a_scales[q] = asc
@@ -124,9 +127,9 @@ def tile_fractalblock_pb_t_kernel(tc, attn_out, x, o_w, norm2_w, scale_gamma, sc
         s1_ps = {}
         x1_t = {}
 
-        def s1_mm(q, jj, halves=(0, 1)):
+        def s1_mm(q, jj, halves=(0, 1), tag="s1"):
             for hf in halves:
-                ps = psum.tile([P, 512], F32, name="s1_ps", tag="s1", bufs=BANKS["s1"])
+                ps = psum.tile([P, 512], F32, name="s1_ps", tag=tag, bufs=BANKS[tag])
                 nc.tensor.matmul_mx(
                     out=ps[:],
                     lhsT=a_codes[q][:, jj * P:(jj + 1) * P].bitcast(FP8X4),
@@ -158,6 +161,7 @@ def tile_fractalblock_pb_t_kernel(tc, attn_out, x, o_w, norm2_w, scale_gamma, sc
         ss_t = {}
         sse_t = {}
         y_t = {}
+        r_t = {}
 
         def sq(q, jj):
             if jj == 0:
@@ -169,18 +173,21 @@ def tile_fractalblock_pb_t_kernel(tc, attn_out, x, o_w, norm2_w, scale_gamma, sc
             sse_t[q] = small.tile([P, 2], F32, name="sse", tag="sse")
             eng.tensor_scalar(out=sse_t[q][:], in0=ss_t[q][:], scalar1=2.0 ** -13, scalar2=None, op0=ALU.add)
 
-        def scale_y(q, on_vector=()):
-            r = small.tile([P, 2], F32, name="r", tag="r")
-            nc.gpsimd.tensor_tensor(out=r[:], in0=sse_t[q][:], in1=neg_half[:], op=ALU.pow)
-            y = work.tile([P, 2, D], F32, name="y", tag="y", bufs=5)
-            for jj in range(2):
-                eng = nc.vector if jj in on_vector else nc.gpsimd
-                eng.tensor_scalar(
-                    out=y[:, jj, :].rearrange("p (t z i) -> p t z i", t=4, i=8),
-                    in0=x1_t[q][:, jj, :].rearrange("p (z t i) -> p t z i", t=4, i=8),
-                    scalar1=r[:, jj:jj + 1], scalar2=0.0, op0=ALU.mult, op1=ALU.add,
-                )
-            y_t[q] = y
+        def rstd(q):
+            r_t[q] = small.tile([P, 2], F32, name="r", tag="r")
+            nc.gpsimd.tensor_tensor(out=r_t[q][:], in0=sse_t[q][:], in1=neg_half[:], op=ALU.pow)
+            y_t[q] = work.tile([P, 2, D], F32, name="y", tag="y", bufs=5)
+
+        def scale_y(q, jj, engine):
+            dst = y_t[q][:, jj, :].rearrange("p (t z i) -> p t z i", t=4, i=8)
+            src = x1_t[q][:, jj, :].rearrange("p (z t i) -> p t z i", t=4, i=8)
+            r = r_t[q][:, jj:jj + 1]
+            if engine == "scalar":
+                nc.scalar.activation(out=dst, in_=src, func=ACT.Copy, scale=r)
+            elif engine == "vector":
+                nc.vector.tensor_scalar(out=dst, in0=src, scalar1=r, scalar2=None, op0=ALU.mult)
+            else:
+                nc.gpsimd.tensor_scalar(out=dst, in0=src, scalar1=r, scalar2=0.0, op0=ALU.mult, op1=ALU.add)
 
         H_t = {}
         hg_t = {}
@@ -282,8 +289,6 @@ def tile_fractalblock_pb_t_kernel(tc, attn_out, x, o_w, norm2_w, scale_gamma, sc
         def w_quant(c):
             nc.vector.quantize_mx(out=w_codes[:, c, :].bitcast(FP8X4), scales=w_scales[:, c, :], in_=wg[:, c, :])
 
-        at_tr(0)
-        at_cp(0, True)
         owg = work.tile([P, 4 * D], BF16, name="owg", tag="hg", align_bytes=64)
         owg_f = owg[:].bitcast(F32)
         ow_f = ow_sb[:].rearrange("p t k -> p (t k)").bitcast(F32)
@@ -308,6 +313,11 @@ def tile_fractalblock_pb_t_kernel(tc, attn_out, x, o_w, norm2_w, scale_gamma, sc
                 in_=owg[:, h * 2048:(h + 1) * 2048],
             )
 
+        warm_ps = psum.tile([P, 512], F32, name="warm_ps", tag="s2", bufs=BANKS["s2"])
+        for i in range(WARM):
+            nc.tensor.matmul(warm_ps[:], zeros[:, 0:P], zeros[:], start=True, stop=True)
+        at_tr(0)
+        at_cp(0, True)
         ow_prep(0, True)
         ow_prep(1, False)
         at_q(0)
@@ -320,19 +330,53 @@ def tile_fractalblock_pb_t_kernel(tc, attn_out, x, o_w, norm2_w, scale_gamma, sc
         s1_add(0, 0, (0,))
         s1_add(0, 1, (0,))
         s1_mm(0, 0, (1,))
-        s1_mm(0, 1, (1,))
-        s1_add(0, 0, (1,))
-        s1_add(0, 1, (1,))
+        s1_mm(0, 1, (1,), "s2")
         at_tr(1)
         at_cp(1, False)
+        s1_add(0, 0, (1,))
+        sq(0, 0)
+        s1_add(0, 1, (1,))
+        sq(0, 1)
+        at_q(1)
+        sse(0, nc.gpsimd)
+        rstd(0)
+        scale_y(0, 1, "gpsimd")
+        s1_mm(1, 0)
+        s1_mm(1, 1)
         nc.vector.tensor_copy(out=vperm[:].rearrange("p (t q i) -> p t q i", t=4, i=8), in_=vec[:].rearrange("p (q t i) -> p t q i", t=4, i=8))
-        for r in range(4):
-            w_perm(r)
         vps = psum.tile([P, 4, P], BF16, name="v_ps", tag="tp", bufs=BANKS["tp"])
         for t in range(4):
             nc.tensor.transpose(vps[:, t, :], vperm[:, t * P:(t + 1) * P], ident_b[:])
+        for r in range(4):
+            w_perm(r)
+        at_tr(2)
+        at_cp(2, False)
+        w_tr(0, 0)
+        s1_add(1, 0)
+        sq(1, 0)
+        s1_add(1, 1)
+        sq(1, 1)
         nc.vector.tensor_copy(out=vcol[:], in_=vps[:, :, 0:6])
         nc.vector.scalar_tensor_tensor(out=g32[:], in0=vcol[:, :, 0:2], scalar=32.0, in1=vcol[:, :, 2:4], op0=ALU.mult, op1=ALU.mult)
+        at_q(2)
+        scale_y(0, 0, "vector")
+        w_tr(0, 1)
+        sse(1, nc.gpsimd)
+        rstd(1)
+        scale_y(1, 1, "gpsimd")
+        s1_mm(2, 0)
+        s1_mm(2, 1)
+        at_tr(3)
+        at_cp(3, False)
+        s1_add(2, 0)
+        w_tr(1, 0)
+        sq(2, 0)
+        s1_add(2, 1)
+        at_q(3)
+        scale_y(1, 0, "vector")
+        w_tr(1, 1)
+        at_tr(4)
+        w_quant(0)
 
         plan = []
 
@@ -344,13 +388,10 @@ def tile_fractalblock_pb_t_kernel(tc, attn_out, x, o_w, norm2_w, scale_gamma, sc
             add(2 * (g - XB) + 3, 0, load, g)
         for q in range(NQ):
             if q >= 1:
-                add(q - 1, 50 if q <= FILL else 11, at_q, q)
+                add(q - 1, 11, at_q, q)
             if q >= 2:
                 add(q - 2, 49, at_tr, q)
-                if q - 2 >= FILL:
-                    add(q - 1, 9.2, at_cp, q, True)
-                else:
-                    add(q - 2, 62, at_cp, q, False)
+                add(q - 1, 3, at_cp, q, False)
             if q >= 1:
                 add(q, 30, s1_mm, q, 0)
                 add(q, 40, s1_mm, q, 1)
@@ -363,7 +404,9 @@ def tile_fractalblock_pb_t_kernel(tc, attn_out, x, o_w, norm2_w, scale_gamma, sc
                     add(q + 1, 5, sse, q, nc.gpsimd)
                 else:
                     add(q + 1, 14, sse, q)
-                add(q + 1, 15, scale_y, q)
+                add(q + 1, 15, rstd, q)
+                add(q + 1, 16, scale_y, q, 1, "gpsimd")
+                add(q + 1, 47, scale_y, q, 0, "vector")
         for g in range(NG - 1):
             a = 2 * g + 3
             for c8 in range(8):
@@ -383,11 +426,8 @@ def tile_fractalblock_pb_t_kernel(tc, attn_out, x, o_w, norm2_w, scale_gamma, sc
                     add(s, (57, 30)[jj], silu, n)
                 if s + 1 - jj < NQ:
                     add(s + 1 - jj, (9.5, 38)[jj], ffmul, n)
-        for i in range(4):
-            add(i // 2, 60 + i % 2, w_tr, i // 2, i % 2)
-            if i % 2 == 1:
-                add(1 + i // 2, 53, w_quant, i // 2)
-        for item in sorted(plan, key=lambda it: (it[0], it[1])):
+        add(4, 9, w_quant, 1)
+        for item in sorted((it for it in plan if it[0] >= FILL), key=lambda it: (it[0], it[1])):
             item[2]()
 
         g = NG - 1
@@ -409,7 +449,9 @@ def tile_fractalblock_pb_t_kernel(tc, attn_out, x, o_w, norm2_w, scale_gamma, sc
         yt_aff(g - 1, 6)
         silu(n - 6)
         yt_aff(g - 1, 7)
-        scale_y(q, (0,))
+        rstd(q)
+        scale_y(q, 1, "gpsimd")
+        scale_y(q, 0, "vector")
         s2_mm(n - 5)
         for c8 in range(4):
             yt_tr(g, c8, 0, 2, ("tp", "s1")[c8 // 3])

@@ -64,10 +64,12 @@ def tile_fractalblock_pb_t_kernel(tc, attn_out, x, o_w, norm2_w, scale_gamma, sc
         x_sb = {}
         at_sb = {}
 
-        def load(g):
+        def load_attn(g):
             a = io.tile([P, 4 * DA], BF16, name="at_sb", tag="at_sb")
             nc.sync.dma_start(out=a[:], in_=attn_f[g * 512:(g + 1) * 512, :].rearrange("(p j) k -> p (j k)", j=4))
             at_sb[g] = a
+
+        def load_x(g):
             xx = io.tile([P, 4, D], BF16, name="x_sb", tag="x_sb")
             nc.sync.dma_start(out=xx[:], in_=x_f[g * 512:(g + 1) * 512, :].rearrange("(p j) d -> p j d", j=4))
             x_sb[g] = xx
@@ -86,11 +88,14 @@ def tile_fractalblock_pb_t_kernel(tc, attn_out, x, o_w, norm2_w, scale_gamma, sc
         nc.sync.dma_start(out=x0[:, 2:4, :], in_=x0_src[:, 2:4, :])
         at_sb[0] = a0
         x_sb[0] = x0
+        load_attn(1)
         w_sb = work.tile([P, 4, D], BF16, name="w_sb", tag="w_sb", bufs=1)
         nc.sync.dma_start(out=w_sb[:, 0:2, :], in_=gate_w.rearrange("(r p) k -> p r k", p=P))
         nc.sync.dma_start(out=w_sb[:, 2:4, :], in_=up_w.rearrange("(r p) k -> p r k", p=P))
-        for g in range(1, XB):
-            load(g)
+        load_x(1)
+        for g in range(2, XB):
+            load_attn(g)
+            load_x(g)
 
         at_ps = {}
         ag_t = {}
@@ -178,9 +183,9 @@ def tile_fractalblock_pb_t_kernel(tc, attn_out, x, o_w, norm2_w, scale_gamma, sc
             nc.gpsimd.tensor_tensor(out=r_t[q][:], in0=sse_t[q][:], in1=neg_half[:], op=ALU.pow)
             y_t[q] = work.tile([P, 2, D], F32, name="y", tag="y", bufs=5)
 
-        def scale_y(q, jj, engine):
-            dst = y_t[q][:, jj, :].rearrange("p (t z i) -> p t z i", t=4, i=8)
-            src = x1_t[q][:, jj, :].rearrange("p (z t i) -> p t z i", t=4, i=8)
+        def scale_y(q, jj, engine, t0=0, t1=4):
+            dst = y_t[q][:, jj, 256 * t0:256 * t1].rearrange("p (t z i) -> p t z i", t=t1 - t0, i=8)
+            src = x1_t[q][:, jj, :].rearrange("p (z t i) -> p t z i", t=4, i=8)[:, t0:t1]
             r = r_t[q][:, jj:jj + 1]
             if engine == "scalar":
                 nc.scalar.activation(out=dst, in_=src, func=ACT.Copy, scale=r)
@@ -336,47 +341,49 @@ def tile_fractalblock_pb_t_kernel(tc, attn_out, x, o_w, norm2_w, scale_gamma, sc
         s1_add(0, 0, (1,))
         sq(0, 0)
         s1_add(0, 1, (1,))
-        sq(0, 1)
+        at_tr(2)
+        at_tr(3)
         at_q(1)
-        sse(0, nc.gpsimd)
-        rstd(0)
-        scale_y(0, 1, "gpsimd")
+        nc.vector.tensor_copy(out=vperm[:].rearrange("p (t q i) -> p t q i", t=4, i=8), in_=vec[:].rearrange("p (q t i) -> p t q i", t=4, i=8))
+        w_perm(0)
+        w_perm(1)
+        at_cp(2, False)
         s1_mm(1, 0)
         s1_mm(1, 1)
-        nc.vector.tensor_copy(out=vperm[:].rearrange("p (t q i) -> p t q i", t=4, i=8), in_=vec[:].rearrange("p (q t i) -> p t q i", t=4, i=8))
+        at_cp(3, False)
+        sq(0, 1)
         vps = psum.tile([P, 4, P], BF16, name="v_ps", tag="tp", bufs=BANKS["tp"])
         for t in range(4):
             nc.tensor.transpose(vps[:, t, :], vperm[:, t * P:(t + 1) * P], ident_b[:])
-        for r in range(4):
-            w_perm(r)
-        at_tr(2)
-        at_cp(2, False)
-        w_tr(0, 0)
         s1_add(1, 0)
-        sq(1, 0)
+        w_tr(0, 0)
+        w_tr(1, 0)
         s1_add(1, 1)
-        sq(1, 1)
-        nc.vector.tensor_copy(out=vcol[:], in_=vps[:, :, 0:6])
-        nc.vector.scalar_tensor_tensor(out=g32[:], in0=vcol[:, :, 0:2], scalar=32.0, in1=vcol[:, :, 2:4], op0=ALU.mult, op1=ALU.mult)
+        sse(0, nc.gpsimd)
+        rstd(0)
         at_q(2)
-        scale_y(0, 0, "vector")
-        w_tr(0, 1)
-        sse(1, nc.gpsimd)
-        rstd(1)
-        scale_y(1, 1, "gpsimd")
+        at_q(3)
+        w_perm(2)
+        w_perm(3)
         s1_mm(2, 0)
         s1_mm(2, 1)
-        at_tr(3)
-        at_cp(3, False)
+        sq(1, 0)
+        nc.vector.tensor_copy(out=vcol[:], in_=vps[:, :, 0:6])
         s1_add(2, 0)
-        w_tr(1, 0)
-        sq(2, 0)
+        sq(1, 1)
         s1_add(2, 1)
-        at_q(3)
-        scale_y(1, 0, "vector")
+        w_tr(0, 1)
         w_tr(1, 1)
+        nc.vector.scalar_tensor_tensor(out=g32[:], in0=vcol[:, :, 0:2], scalar=32.0, in1=vcol[:, :, 2:4], op0=ALU.mult, op1=ALU.mult)
+        scale_y(0, 0, "vector")
+        scale_y(0, 1, "vector")
+        sse(1, nc.gpsimd)
+        rstd(1)
         at_tr(4)
+        sq(2, 0)
         w_quant(0)
+
+        scale_y(1, 1, "vector", 2, 4)
 
         plan = []
 
@@ -385,28 +392,25 @@ def tile_fractalblock_pb_t_kernel(tc, attn_out, x, o_w, norm2_w, scale_gamma, sc
 
         FILL = 3
         for g in range(XB, NG):
-            add(2 * (g - XB) + 3, 0, load, g)
+            add(2 * (g - XB) + 3, 0, load_attn, g)
+            add(2 * (g - XB) + 3, 0.5, load_x, g)
         for q in range(NQ):
-            if q >= 1:
-                add(q - 1, 11, at_q, q)
-            if q >= 2:
-                add(q - 2, 49, at_tr, q)
-                add(q - 1, 3, at_cp, q, False)
-            if q >= 1:
-                add(q, 30, s1_mm, q, 0)
-                add(q, 40, s1_mm, q, 1)
-                add(q, 35, s1_add, q, 0)
-                add(q, 45, s1_add, q, 1)
+            add(q - 1, 11, at_q, q)
+            add(q - 2, 49, at_tr, q)
+            add(q - 1, 3, at_cp, q, False)
+            add(q, 30, s1_mm, q, 0)
+            add(q, 40, s1_mm, q, 1)
+            add(q, 35, s1_add, q, 0)
+            add(q, 45, s1_add, q, 1)
             add(q, 55, sq, q, 0)
-            if q < NQ - 1:
+            if q + 1 < NQ:
                 add(q + 1, 4, sq, q, 1)
-                if q < FILL:
-                    add(q + 1, 5, sse, q, nc.gpsimd)
-                else:
-                    add(q + 1, 14, sse, q)
+                add(q + 1, 14, sse, q)
                 add(q + 1, 15, rstd, q)
-                add(q + 1, 16, scale_y, q, 1, "gpsimd")
-                add(q + 1, 47, scale_y, q, 0, "vector")
+                add(q + 1, 16, scale_y, q, 1, "gpsimd", 2, 4)
+            if q + 2 < NQ:
+                add(q + 2, 8, scale_y, q, 0, "vector")
+                add(q + 2, 8.5, scale_y, q, 1, "vector", 0, 2)
         for g in range(NG - 1):
             a = 2 * g + 3
             for c8 in range(8):
@@ -433,71 +437,82 @@ def tile_fractalblock_pb_t_kernel(tc, attn_out, x, o_w, norm2_w, scale_gamma, sc
         g = NG - 1
         q = NQ - 1
         n = 4 * g
+        scale_y(q - 1, 0, "vector")
+        scale_y(q - 1, 1, "vector", 0, 2)
         ffmul(n - 8)
         s2_mm(n - 7)
         for c8 in range(4, 8):
             yt_tr(g - 1, c8, 0, 4, ("tp", "s1")[c8 // 7])
+        for c8 in range(2):
+            yt_tr(g, c8, 0, 2, "s1")
         sq(q, 1)
-        regroup(g - 1, 0, 0, 512)
         silu(n - 7)
+        regroup(g - 1, 0, 0, 512)
+        for c8 in range(4, 8):
+            yt_aff(g - 1, c8)
         hquant(g - 1, 0, 0, 512)
-        yt_aff(g - 1, 4, on_vector=True)
-        yt_aff(g - 1, 5)
-        s2_mm(n - 6)
         sse(q)
-        ffmul(n - 7)
-        yt_aff(g - 1, 6)
-        silu(n - 6)
-        yt_aff(g - 1, 7)
         rstd(q)
-        scale_y(q, 1, "gpsimd")
+        ffmul(n - 7)
+        s2_mm(n - 6)
+        for c8 in range(2, 5):
+            yt_tr(g, c8, 0, 2, "tp")
         scale_y(q, 0, "vector")
-        s2_mm(n - 5)
-        for c8 in range(4):
-            yt_tr(g, c8, 0, 2, ("tp", "s1")[c8 // 3])
-            yt_aff(g, c8, 0, 2, c8 < 2)
-        ffmul(n - 6)
-        silu(n - 5)
+        scale_y(q, 1, "vector")
+        for c8 in range(2):
+            yt_aff(g, c8, 0, 2)
+        silu(n - 6)
         regroup(g - 1, 1, 0, 512)
-        for c8 in range(4, 8):
-            yt_tr(g, c8, 0, 2, ("s1", "tp")[c8 // 6])
-        regroup(g, 0, 0, 256)
+        s2_mm(n - 5)
+        for c8 in range(5, 8):
+            yt_tr(g, c8, 0, 2, "s1")
+        for c8 in range(2, 4):
+            yt_aff(g, c8, 0, 2)
+        ffmul(n - 6)
         hquant(g - 1, 1, 0, 512)
-        for c8 in range(4, 8):
+        silu(n - 5)
+        for c8 in range(4, 6):
+            yt_aff(g, c8, 0, 2)
+        regroup(g, 0, 0, 256)
+        for c8 in range(0, 3):
+            yt_tr(g, c8, 2, 4, "tp")
+        s2_mm(n - 4)
+        for c8 in range(6, 8):
             yt_aff(g, c8, 0, 2)
         ffmul(n - 5)
         hquant(g, 0, 0, 256)
-        s2_mm(n - 4)
-        s2_mm(n - 3)
+        yt_tr(g, 3, 2, 4, "s1")
+        yt_tr(g, 4, 2, 4, "s1")
         silu(n - 4)
-        for c8 in range(0, 4):
-            yt_tr(g, c8, 2, 4, ("tp", "s1")[c8 // 2])
-            yt_aff(g, c8, 2, 4, c8 % 2 == 1)
-        silu(n - 3)
-        ffmul(n - 4)
+        s2_mm(n - 3)
         regroup(g, 1, 0, 256)
-        for c8 in range(4, 8):
-            yt_tr(g, c8, 2, 4, ("tp", "s1")[c8 // 6])
-            yt_aff(g, c8, 2, 4, c8 % 2 == 1)
+        for c8 in range(0, 4):
+            yt_aff(g, c8, 2, 4, c8 == 3)
+        ffmul(n - 4)
         hquant(g, 1, 0, 256)
+        silu(n - 3)
+        for c8 in range(5, 8):
+            yt_tr(g, c8, 2, 4, "tp")
+        for c8 in range(4, 8):
+            yt_aff(g, c8, 2, 4, c8 % 2 == 0)
         regroup(g, 0, 256, 512)
-        regroup(g, 1, 256, 512)
-        ffmul(n - 3)
-        hquant(g, 0, 256, 512)
-        hquant(g, 1, 256, 512)
         s2_mm(n - 2)
+        ffmul(n - 3)
         silu(n - 2)
-        s2_mm(n - 1, "s1")
+        hquant(g, 0, 256, 512)
+        regroup(g, 1, 256, 512)
+        s2_mm(n - 1)
         silu(n - 1)
+        ffmul(n - 2)
+        hquant(g, 1, 256, 512)
+        ffmul(n - 1)
         s2_mm(n, "s1")
         silu(n)
         s2_mm(n + 1, "s1")
         silu(n + 1)
+        ffmul(n, 2)
         s2_mm(n + 2)
         silu(n + 2)
-        ffmul(n - 2)
-        ffmul(n - 1)
-        ffmul(n, 2)
         ffmul(n + 1, 2)
         s2_mm(n + 3)
         silu(n + 3)

@@ -204,6 +204,8 @@ def tile_fractalblock_pb_t_kernel(tc, attn_out, x, o_w, norm2_w, scale_gamma, sc
             c, t = divmod(c8, 4)
             k0 = (2 * t + c) * P
             ps = psum.tile([P, j1 - j0, P], F32, name="yt_ps", tag=tag, bufs=BANKS[tag])
+            if c8 % 2 == 1:
+                nc.tensor.matmul(ps[:].rearrange("p j m -> p (j m)"), zeros[:, 0:P], zeros[:, 0:(j1 - j0) * P], start=True, stop=True)
             for j in range(j0, j1):
                 nc.tensor.transpose(ps[:, j - j0, :], y_t[2 * g + j // 2][:, j % 2, k0:k0 + P], ident_f[:])
             yt_ps[(g, c8, j0)] = ps

@@ -330,22 +330,22 @@ def tile_fractalblock_pb_t_kernel(tc, attn_out, x, o_w, norm2_w, scale_gamma, sc
         at_q(0)
         ow_prep(2, False)
         ow_quant(0)
-        ow_prep(3, True)
+        ow_prep(3, False)
         s1_mm(0, 0, (0,))
         s1_mm(0, 1, (0,))
+        at_tr(1)
+        at_cp(1, False)
         ow_quant(1)
         s1_add(0, 0, (0,))
         s1_add(0, 1, (0,))
         s1_mm(0, 0, (1,))
         s1_mm(0, 1, (1,), "s2")
-        at_tr(1)
-        at_cp(1, False)
         s1_add(0, 0, (1,))
         sq(0, 0)
+        at_q(1)
         s1_add(0, 1, (1,))
         at_tr(2)
         at_tr(3)
-        at_q(1)
         nc.vector.tensor_copy(out=vperm[:].rearrange("p (t q i) -> p t q i", t=4, i=8), in_=vec[:].rearrange("p (q t i) -> p t q i", t=4, i=8))
         w_perm(0)
         w_perm(1)
@@ -385,7 +385,7 @@ def tile_fractalblock_pb_t_kernel(tc, attn_out, x, o_w, norm2_w, scale_gamma, sc
         sq(2, 0)
         w_quant(0)
 
-        scale_y(1, 1, "vector", 2, 4)
+        scale_y(1, 1, "vector", 1, 4)
 
         plan = []
 
@@ -401,7 +401,10 @@ def tile_fractalblock_pb_t_kernel(tc, attn_out, x, o_w, norm2_w, scale_gamma, sc
             add(q - 2, 49, at_tr, q)
             add(q - 1, 3, at_cp, q, False)
             add(q, 30, s1_mm, q, 0)
-            add(q, 40, s1_mm, q, 1)
+            if q in (3, 4):
+                add(q, 30.5, s1_mm, q, 1, (0, 1), "s2")
+            else:
+                add(q, 40, s1_mm, q, 1)
             add(q, 35, s1_add, q, 0)
             add(q, 45, s1_add, q, 1)
             add(q, 55, sq, q, 0)
@@ -409,10 +412,10 @@ def tile_fractalblock_pb_t_kernel(tc, attn_out, x, o_w, norm2_w, scale_gamma, sc
                 add(q + 1, 4, sq, q, 1)
                 add(q + 1, 14, sse, q)
                 add(q + 1, 15, rstd, q)
-                add(q + 1, 16, scale_y, q, 1, "gpsimd", 2, 4)
+                add(q + 1, 16, scale_y, q, 1, "gpsimd", 1, 4)
             if q + 2 < NQ:
                 add(q + 2, 8, scale_y, q, 0, "vector")
-                add(q + 2, 8.5, scale_y, q, 1, "vector", 0, 2)
+                add(q + 2, 8.5, scale_y, q, 1, "vector", 0, 1)
         for g in range(NG - 1):
             a = 2 * g + 3
             for c8 in range(8):
@@ -440,7 +443,7 @@ def tile_fractalblock_pb_t_kernel(tc, attn_out, x, o_w, norm2_w, scale_gamma, sc
         q = NQ - 1
         n = 4 * g
         scale_y(q - 1, 0, "vector")
-        scale_y(q - 1, 1, "vector", 0, 2)
+        scale_y(q - 1, 1, "vector", 0, 1)
         ffmul(n - 8)
         s2_mm(n - 7)
         for c8 in range(4, 8):

@@ -204,7 +204,7 @@ def tile_fractalblock_pb_t_kernel(tc, attn_out, x, o_w, norm2_w, scale_gamma, sc
             c, t = divmod(c8, 4)
             k0 = (2 * t + c) * P
             ps = psum.tile([P, j1 - j0, P], F32, name="yt_ps", tag=tag, bufs=BANKS[tag])
-            if c8 % 2 == 1:
+            if c8 % 4 != 0 and g < NG - 1:
                 nc.tensor.matmul(ps[:].rearrange("p j m -> p (j m)"), zeros[:, 0:P], zeros[:, 0:(j1 - j0) * P], start=True, stop=True)
             for j in range(j0, j1):
                 nc.tensor.transpose(ps[:, j - j0, :], y_t[2 * g + j // 2][:, j % 2, k0:k0 + P], ident_f[:])
@@ -260,7 +260,7 @@ def tile_fractalblock_pb_t_kernel(tc, attn_out, x, o_w, norm2_w, scale_gamma, sc
             gu_t[n] = gu
 
         def silu(n):
-            sg = work.tile([P, FF], F32, name="sg", tag="sg", bufs=3)
+            sg = work.tile([P, FF], F32, name="sg", tag="sg", bufs=6)
             nc.scalar.activation(out=sg[:], in_=gu_t[n][:, 0:FF], func=ACT.Silu)
             sg_t[n] = sg
 
@@ -455,10 +455,10 @@ def tile_fractalblock_pb_t_kernel(tc, attn_out, x, o_w, norm2_w, scale_gamma, sc
         regroup(g - 1, 0, 0, 512)
         for c8 in range(4, 8):
             yt_aff(g - 1, c8)
-        hquant(g - 1, 0, 0, 512)
         sse(q)
         rstd(q)
         ffmul(n - 7)
+        hquant(g - 1, 0, 0, 512)
         s2_mm(n - 6)
         for c8 in range(2, 5):
             yt_tr(g, c8, 0, 2, "tp")
@@ -499,27 +499,27 @@ def tile_fractalblock_pb_t_kernel(tc, attn_out, x, o_w, norm2_w, scale_gamma, sc
         for c8 in range(5, 8):
             yt_tr(g, c8, 2, 4, "tp")
         for c8 in range(4, 8):
-            yt_aff(g, c8, 2, 4, c8 % 2 == 0)
+            yt_aff(g, c8, 2, 4)
         regroup(g, 0, 256, 512)
         s2_mm(n - 2)
         ffmul(n - 3)
         silu(n - 2)
         hquant(g, 0, 256, 512)
         regroup(g, 1, 256, 512)
-        s2_mm(n - 1)
-        silu(n - 1)
-        ffmul(n - 2)
-        hquant(g, 1, 256, 512)
-        ffmul(n - 1)
+        s2_mm(n - 1, "s1")
         s2_mm(n, "s1")
-        silu(n)
         s2_mm(n + 1, "s1")
+        ffmul(n - 2)
+        silu(n - 1)
+        silu(n)
         silu(n + 1)
-        ffmul(n, 2)
-        s2_mm(n + 2)
+        hquant(g, 1, 256, 512)
+        s2_mm(n + 2, "tp")
+        s2_mm(n + 3, "tp")
         silu(n + 2)
-        ffmul(n + 1, 2)
-        s2_mm(n + 3)
         silu(n + 3)
+        ffmul(n - 1)
+        ffmul(n, 2)
+        ffmul(n + 1, 2)
         ffmul(n + 2, 1)
         ffmul(n + 3, 1)

@@ -81,8 +81,8 @@ def tile_fractalblock_pb_t_kernel(tc, attn_out, x, o_w, norm2_w, scale_gamma, sc
         x0 = io.tile([P, 4, D], BF16, name="x_sb", tag="x_sb")
         x0_src = x_f[0:512, :].rearrange("(p j) d -> p j d", j=4)
         nc.sync.dma_start(out=a0[:, 0:1024], in_=a0_src[:, 0:1024])
-        nc.sync.dma_start(out=ow_sb[:, 0:4, :], in_=ow_src[:, 0:4, :])
-        nc.sync.dma_start(out=ow_sb[:, 4:8, :], in_=ow_src[:, 4:8, :])
+        for b in range(4):
+            nc.sync.dma_start(out=ow_sb[:, 2 * b:2 * b + 2, :], in_=ow_src[:, 2 * b:2 * b + 2, :])
         nc.sync.dma_start(out=x0[:, 0:2, :], in_=x0_src[:, 0:2, :])
         nc.sync.dma_start(out=a0[:, 1024:2048], in_=a0_src[:, 1024:2048])
         nc.sync.dma_start(out=x0[:, 2:4, :], in_=x0_src[:, 2:4, :])
@@ -204,7 +204,7 @@ def tile_fractalblock_pb_t_kernel(tc, attn_out, x, o_w, norm2_w, scale_gamma, sc
             c, t = divmod(c8, 4)
             k0 = (2 * t + c) * P
             ps = psum.tile([P, j1 - j0, P], F32, name="yt_ps", tag=tag, bufs=BANKS[tag])
-            if c8 % 4 != 0 and g < NG - 1:
+            for i in range(2 if c8 % 4 == 2 and g < NG - 1 else 0):
                 nc.tensor.matmul(ps[:].rearrange("p j m -> p (j m)"), zeros[:, 0:P], zeros[:, 0:(j1 - j0) * P], start=True, stop=True)
             for j in range(j0, j1):
                 nc.tensor.transpose(ps[:, j - j0, :], y_t[2 * g + j // 2][:, j % 2, k0:k0 + P], ident_f[:])

@@ -19,7 +19,7 @@ FF = 256
 NQ = NTOK // (2 * P)
 NG = NQ // 2
 FLOPS = 2 * NTOK * DA * D + 2 * NTOK * D * 2 * FF
-WARM = 6
+WARM = 5
 XB = 5
 BANKS = {"tp": 3, "s1": 3, "s2": 2}
 
@@ -39,21 +39,21 @@ def tile_fractalblock_pb_t_kernel(tc, attn_out, x, o_w, norm2_w, scale_gamma, sc
         psum = ctx.enter_context(tc.psum_pool(name="psum", bufs=2))
         ctx.enter_context(tc.manual_schedule())
 
+        vec = const.tile([P, 512], BF16, name="vec")
+        nc.vector.memset(vec[:], 0.0)
+        for v, src in enumerate((norm2_w, scale_gamma, scale_beta)):
+            nc.scalar.dma_start(out=vec[2 * v:2 * v + 2, :], in_=src.rearrange("(c k) -> c k", k=512))
+        vperm = const.tile([P, 512], BF16, name="vperm")
+        zeros = const.tile([P, 512], BF16, name="zeros")
+        nc.gpsimd.memset(zeros[:], 0.0)
         ident_f = const.tile([P, P], F32, name="ident_f")
         make_identity(nc, ident_f[:])
         ident_b = const.tile([P, P], BF16, name="ident_b")
         make_identity(nc, ident_b[:])
         neg_half = const.tile([P, 2], F32, name="neg_half")
         nc.vector.memset(neg_half[:], -0.5)
-        vec = const.tile([P, 512], BF16, name="vec")
-        nc.vector.memset(vec[:], 0.0)
-        for v, src in enumerate((norm2_w, scale_gamma, scale_beta)):
-            nc.scalar.dma_start(out=vec[2 * v:2 * v + 2, :], in_=src.rearrange("(c k) -> c k", k=512))
-        vperm = const.tile([P, 512], BF16, name="vperm")
         warm = const.tile([P, 1], F32, name="warm")
         nc.scalar.activation(out=warm[:], in_=neg_half[:, 0:1], func=ACT.Silu)
-        zeros = const.tile([P, 512], BF16, name="zeros")
-        nc.vector.memset(zeros[:], 0.0)
         vcol = const.tile([P, 4, 6], F32, name="vcol")
         g32 = const.tile([P, 4, 2], F32, name="g32")
         ow_codes = const.tile([P, D], U32, name="ow_codes", align_bytes=64)

from contextlib import ExitStack

import concourse.mybir as mybir
from concourse.masks import make_identity

F32 = mybir.dt.float32
BF16 = mybir.dt.bfloat16
U32 = mybir.dt.uint32
U8 = mybir.dt.uint8
FP8X4 = mybir.dt.float8_e4m3fn_x4
ALU = mybir.AluOpType
ACT = mybir.ActivationFunctionType

P = 128
NTOK = 4096
DA = 512
D = 1024
FF = 256
NQ = NTOK // (2 * P)
NG = NQ // 2
FLOPS = 2 * NTOK * DA * D + 2 * NTOK * D * 2 * FF
WARM = 5
XB = 5
BANKS = {"tp": 3, "s1": 3, "s2": 2}


def tile_fractalblock_pb_t_kernel(tc, attn_out, x, o_w, norm2_w, scale_gamma, scale_beta, gate_w, up_w, out_0, out_1):
    nc = tc.nc
    attn_f = attn_out.flatten_outer_dims()
    x_f = x.flatten_outer_dims()
    o0_f = out_0.flatten_outer_dims()
    o1_f = out_1.flatten_outer_dims()

    with ExitStack() as ctx:
        const = ctx.enter_context(tc.tile_pool(name="const", bufs=1))
        io = ctx.enter_context(tc.tile_pool(name="io", bufs=XB))
        work = ctx.enter_context(tc.tile_pool(name="work", bufs=2))
        small = ctx.enter_context(tc.tile_pool(name="small", bufs=4))
        psum = ctx.enter_context(tc.psum_pool(name="psum", bufs=2))
        ctx.enter_context(tc.manual_schedule())

        vec = const.tile([P, 512], BF16, name="vec")
        nc.vector.memset(vec[:], 0.0)
        for v, src in enumerate((norm2_w, scale_gamma, scale_beta)):
            nc.scalar.dma_start(out=vec[2 * v:2 * v + 2, :], in_=src.rearrange("(c k) -> c k", k=512))
        vperm = const.tile([P, 512], BF16, name="vperm")
        zeros = const.tile([P, 512], BF16, name="zeros")
        nc.gpsimd.memset(zeros[:], 0.0)
        ident_f = const.tile([P, P], F32, name="ident_f")
        make_identity(nc, ident_f[:])
        ident_b = const.tile([P, P], BF16, name="ident_b")
        make_identity(nc, ident_b[:])
        neg_half = const.tile([P, 2], F32, name="neg_half")
        nc.vector.memset(neg_half[:], -0.5)
        warm = const.tile([P, 1], F32, name="warm")
        nc.scalar.activation(out=warm[:], in_=neg_half[:, 0:1], func=ACT.Silu)
        vcol = const.tile([P, 4, 6], F32, name="vcol")
        g32 = const.tile([P, 4, 2], F32, name="g32")
        ow_codes = const.tile([P, D], U32, name="ow_codes", align_bytes=64)
        ow_scales = const.tile([P, D], U8, name="ow_scales", align_bytes=64)
        w_codes = const.tile([P, 2, 512], U32, name="w_codes", align_bytes=64)
        w_scales = const.tile([P, 2, 512], U8, name="w_scales", align_bytes=64)

        x_sb = {}
        at_sb = {}

        def load_attn(g):
            a = io.tile([P, 4 * DA], BF16, name="at_sb", tag="at_sb")
            nc.sync.dma_start(out=a[:], in_=attn_f[g * 512:(g + 1) * 512, :].rearrange("(p j) k -> p (j k)", j=4))
            at_sb[g] = a

        def load_x(g):
            xx = io.tile([P, 4, D], BF16, name="x_sb", tag="x_sb")
            nc.sync.dma_start(out=xx[:], in_=x_f[g * 512:(g + 1) * 512, :].rearrange("(p j) d -> p j d", j=4))
            x_sb[g] = xx

        a0 = io.tile([P, 4 * DA], BF16, name="at_sb", tag="at_sb")
        a0_src = attn_f[0:512, :].rearrange("(p j) k -> p (j k)", j=4)
        ow_sb = work.tile([P, 8, DA], BF16, name="ow_sb", tag="H")
        ow_src = o_w.rearrange("(t p) k -> p t k", p=P)
        x0 = io.tile([P, 4, D], BF16, name="x_sb", tag="x_sb")
        x0_src = x_f[0:512, :].rearrange("(p j) d -> p j d", j=4)
        nc.sync.dma_start(out=a0[:, 0:1024], in_=a0_src[:, 0:1024])
        for b in range(4):
            nc.sync.dma_start(out=ow_sb[:, 2 * b:2 * b + 2, :], in_=ow_src[:, 2 * b:2 * b + 2, :])
        nc.sync.dma_start(out=x0[:, 0:2, :], in_=x0_src[:, 0:2, :])
        nc.sync.dma_start(out=a0[:, 1024:2048], in_=a0_src[:, 1024:2048])
        nc.sync.dma_start(out=x0[:, 2:4, :], in_=x0_src[:, 2:4, :])
        at_sb[0] = a0
        x_sb[0] = x0
        load_attn(1)
        w_sb = work.tile([P, 4, D], BF16, name="w_sb", tag="w_sb", bufs=1)
        nc.sync.dma_start(out=w_sb[:, 0:2, :], in_=gate_w.rearrange("(r p) k -> p r k", p=P))
        nc.sync.dma_start(out=w_sb[:, 2:4, :], in_=up_w.rearrange("(r p) k -> p r k", p=P))
        load_x(1)
        for g in range(2, XB):
            load_attn(g)
            load_x(g)

        at_ps = {}
        ag_t = {}
        a_codes = {}
        a_scales = {}

        def at_tr(q):
            g, pi = divmod(q, 2)
            af = at_sb[g][:].bitcast(F32)
            ps = psum.tile([P, 2, 2, P], F32, name="at_ps", tag="tp", bufs=BANKS["tp"])
            for jj in range(2):
                for u in range(2):
                    c0 = (2 * pi + jj) * 256
                    nc.tensor.transpose(ps[:, jj, u, :], af[:, c0 + u:c0 + 256:2], ident_f[:])
            at_ps[q] = ps

        def at_cp(q, on_vector):
            ag = work.tile([P, 1024], BF16, name="ag", tag="ag", bufs=3, align_bytes=64)
            dst = ag[:].bitcast(F32).rearrange("p (t m u) -> p t m u", t=2, u=2)
            src = at_ps[q][:].rearrange("p t u m -> p t m u")
            if on_vector:
                nc.vector.tensor_copy(out=dst, in_=src)
            else:
                nc.scalar.copy(out=dst, in_=src)
            ag_t[q] = ag

        def at_q(q):
            ac = work.tile([P, 256], U32, name="ac", tag="ac", bufs=4, align_bytes=64)
            asc = work.tile([P, 256], U8, name="asc", tag="asc", bufs=4, align_bytes=64)
            nc.vector.quantize_mx(out=ac[:].bitcast(FP8X4), scales=asc[:], in_=ag_t[q][:])
            a_codes[q] = ac
            a_scales[q] = asc

        s1_ps = {}
        x1_t = {}

        def s1_mm(q, jj, halves=(0, 1), tag="s1"):
            for hf in halves:
                ps = psum.tile([P, 512], F32, name="s1_ps", tag=tag, bufs=BANKS[tag])
                nc.tensor.matmul_mx(
                    out=ps[:],
                    lhsT=a_codes[q][:, jj * P:(jj + 1) * P].bitcast(FP8X4),
                    lhsT_scale=a_scales[q][:, jj * P:(jj + 1) * P],
                    rhs=ow_codes[:, hf * 512:(hf + 1) * 512].bitcast(FP8X4),
                    rhs_scale=ow_scales[:, hf * 512:(hf + 1) * 512],
                    start=True,
                    stop=True,
                )
                s1_ps[(q, jj, hf)] = ps

        def s1_add(q, jj, halves=(0, 1)):
            g, pi = divmod(q, 2)
            if jj == 0 and halves[0] == 0:
                x1_t[q] = work.tile([P, 2, D], F32, name="x1", tag="x1", bufs=4)
            for hf in halves:
                nc.vector.tensor_tensor(
                    out=x1_t[q][:, jj, hf * 512:(hf + 1) * 512],
                    in0=s1_ps[(q, jj, hf)][:],
                    in1=x_sb[g][:, 2 * pi + jj, hf * 512:(hf + 1) * 512],
                    op=ALU.add,
                )
            if jj == 1 and halves[-1] == 1:
                nc.sync.dma_start(
                    out=o0_f[g * 512:(g + 1) * 512, :].rearrange("(p j) d -> p j d", j=4)[:, 2 * pi:2 * pi + 2, :],
                    in_=x1_t[q][:],
                )

        ss_t = {}
        sse_t = {}
        y_t = {}
        r_t = {}

        def sq(q, jj):
            if jj == 0:
                ss_t[q] = small.tile([P, 2], F32, name="ss", tag="ss")
            junk = work.tile([P, D], BF16, name="junk", tag="junk", bufs=2)
            nc.scalar.activation(out=junk[:], in_=x1_t[q][:, jj, :], func=ACT.Square, accum_out=ss_t[q][:, jj:jj + 1])

        def sse(q, eng=nc.vector):
            sse_t[q] = small.tile([P, 2], F32, name="sse", tag="sse")
            eng.tensor_scalar(out=sse_t[q][:], in0=ss_t[q][:], scalar1=2.0 ** -13, scalar2=None, op0=ALU.add)

        def rstd(q):
            r_t[q] = small.tile([P, 2], F32, name="r", tag="r")
            nc.gpsimd.tensor_tensor(out=r_t[q][:], in0=sse_t[q][:], in1=neg_half[:], op=ALU.pow)
            y_t[q] = work.tile([P, 2, D], F32, name="y", tag="y", bufs=5)

        def scale_y(q, jj, engine, t0=0, t1=4):
            dst = y_t[q][:, jj, 256 * t0:256 * t1].rearrange("p (t z i) -> p t z i", t=t1 - t0, i=8)
            src = x1_t[q][:, jj, :].rearrange("p (z t i) -> p t z i", t=4, i=8)[:, t0:t1]
            r = r_t[q][:, jj:jj + 1]
            if engine == "scalar":
                nc.scalar.activation(out=dst, in_=src, func=ACT.Copy, scale=r)
            elif engine == "vector":
                nc.vector.tensor_scalar(out=dst, in0=src, scalar1=r, scalar2=None, op0=ALU.mult)
            else:
                nc.gpsimd.tensor_scalar(out=dst, in0=src, scalar1=r, scalar2=0.0, op0=ALU.mult, op1=ALU.add)

        H_t = {}
        hg_t = {}
        h_codes = {}
        h_scales = {}
        yt_ps = {}

        def yt_tr(g, c8, j0=0, j1=4, tag="tp"):
            c, t = divmod(c8, 4)
            k0 = (2 * t + c) * P
            ps = psum.tile([P, j1 - j0, P], F32, name="yt_ps", tag=tag, bufs=BANKS[tag])
            for i in range(2 if c8 % 4 == 2 and g < NG - 1 else 0):
                nc.tensor.matmul(ps[:].rearrange("p j m -> p (j m)"), zeros[:, 0:P], zeros[:, 0:(j1 - j0) * P], start=True, stop=True)
            for j in range(j0, j1):
                nc.tensor.transpose(ps[:, j - j0, :], y_t[2 * g + j // 2][:, j % 2, k0:k0 + P], ident_f[:])
            yt_ps[(g, c8, j0)] = ps

        def yt_aff(g, c8, j0=0, j1=4, on_vector=False):
            if c8 == 0 and j0 == 0:
                H_t[g] = work.tile([P, 8, 512], BF16, name="H", tag="H")
            src = yt_ps[(g, c8, j0)][:].rearrange("p j m -> p (j m)")
            c, t = divmod(c8, 4)
            scale = g32[:, t, c:c + 1]
            bias = vcol[:, t, 4 + c:5 + c]
            dst = H_t[g][:, c8, j0 * P:j1 * P]
            if on_vector:
                nc.vector.tensor_scalar(
                    out=dst, in0=src, scalar1=scale, scalar2=bias, op0=ALU.mult, op1=ALU.add,
                )
            else:
                nc.scalar.activation(out=dst, in_=src, func=ACT.Identity, scale=scale, bias=bias)

        def regroup(g, c, m0, m1):
            if c == 0 and m0 == 0:
                hg_t[g] = work.tile([P, 2, 2048], BF16, name="hg", tag="hg", align_bytes=64)
            dst = hg_t[g][:, c, 4 * m0:4 * m1].rearrange("p (m t) -> p m t", t=4).rearrange("p (c i) t -> p c t i", i=4)
            src = H_t[g][:, 4 * c:4 * c + 4, m0:m1].rearrange("p t (c i) -> p c t i", i=4)
            nc.vector.tensor_copy(out=dst, in_=src)

        def hquant(g, c, m0, m1):
            if c == 0 and m0 == 0:
                h_codes[g] = work.tile([P, 2, 512], U32, name="hc", tag="hc", bufs=2, align_bytes=64)
                h_scales[g] = work.tile([P, 2, 512], U8, name="hs", tag="hs", bufs=2, align_bytes=64)
            nc.vector.quantize_mx(
                out=h_codes[g][:, c, m0:m1].bitcast(FP8X4), scales=h_scales[g][:, c, m0:m1], in_=hg_t[g][:, c, 4 * m0:4 * m1]
            )

        gu_t = {}
        sg_t = {}
        ff_t = {}

        def s2_mm(n, tag="s2"):
            g, j = divmod(n, 4)
            gu = psum.tile([P, 2 * FF], F32, name="gu_ps", tag=tag, bufs=BANKS[tag])
            for c in range(2):
                nc.tensor.matmul_mx(
                    out=gu[:],
                    lhsT=h_codes[g][:, c, j * P:(j + 1) * P].bitcast(FP8X4),
                    lhsT_scale=h_scales[g][:, c, j * P:(j + 1) * P],
                    rhs=w_codes[:, c, :].bitcast(FP8X4),
                    rhs_scale=w_scales[:, c, :],
                    start=(c == 0),
                    stop=(c == 1),
                )
            gu_t[n] = gu

        def silu(n):
            sg = work.tile([P, FF], F32, name="sg", tag="sg", bufs=6)
            nc.scalar.activation(out=sg[:], in_=gu_t[n][:, 0:FF], func=ACT.Silu)
            sg_t[n] = sg

        def ffmul(n, store_tiles=4):
            g, j = divmod(n, 4)
            if j == 0:
                ff_t[g] = work.tile([P, 4, FF], F32, name="ff", tag="ff", bufs=2)
            nc.vector.tensor_tensor(out=ff_t[g][:, j, :], in0=gu_t[n][:, FF:2 * FF], in1=sg_t[n][:], op=ALU.mult)
            if j % store_tiles == store_tiles - 1:
                dst = o1_f[g * 512:(g + 1) * 512, :].rearrange("(p j) f -> p j f", j=4)
                j0 = j + 1 - store_tiles
                nc.sync.dma_start(out=dst[:, j0:j + 1, :], in_=ff_t[g][:, j0:j + 1, :])

        wp = work.tile([P, 4, D], BF16, name="wp", tag="wp", bufs=1)
        wg = work.tile([P, 2, 2048], BF16, name="wg", tag="hg", align_bytes=64)
        w_ps = {}

        def w_perm(r):
            nc.vector.tensor_copy(
                out=wp[:, r, :].rearrange("p (t z i) -> p t z i", t=4, i=8),
                in_=w_sb[:, r, :].rearrange("p (z t i) -> p t z i", t=4, i=8),
            )

        def w_tr(c, rp):
            ps = psum.tile([P, 2, 4, P], BF16, name="w_ps", tag="tp", bufs=BANKS["tp"])
            for rr in range(2):
                for t in range(4):
                    k0 = (2 * t + c) * P
                    nc.tensor.transpose(ps[:, rr, t, :], wp[:, 2 * rp + rr, k0:k0 + P], ident_b[:])
            dst = wg[:, c, rp * 1024:(rp + 1) * 1024].rearrange("p (r f t) -> p r f t", r=2, t=4)
            nc.scalar.copy(out=dst, in_=ps[:].rearrange("p r t f -> p r f t"))

        def w_quant(c):
            nc.vector.quantize_mx(out=w_codes[:, c, :].bitcast(FP8X4), scales=w_scales[:, c, :], in_=wg[:, c, :])

        owg = work.tile([P, 4 * D], BF16, name="owg", tag="hg", align_bytes=64)
        owg_f = owg[:].bitcast(F32)
        ow_f = ow_sb[:].rearrange("p t k -> p (t k)").bitcast(F32)

        def ow_prep(b, on_vector):
            ps = psum.tile([P, 2, 2, P], F32, name="ow_ps", tag="tp", bufs=BANKS["tp"])
            for tt in range(2):
                for u in range(2):
                    c0 = (2 * b + tt) * 256
                    nc.tensor.transpose(ps[:, tt, u, :], ow_f[:, c0 + u:c0 + 256:2], ident_f[:])
            dst = owg_f[:, b * 512:(b + 1) * 512].rearrange("p (t m u) -> p t m u", t=2, u=2)
            src = ps[:].rearrange("p t u m -> p t m u")
            if on_vector:
                nc.vector.tensor_copy(out=dst, in_=src)
            else:
                nc.scalar.copy(out=dst, in_=src)

        def ow_quant(h):
            nc.vector.quantize_mx(
                out=ow_codes[:, h * 512:(h + 1) * 512].bitcast(FP8X4),
                scales=ow_scales[:, h * 512:(h + 1) * 512],
                in_=owg[:, h * 2048:(h + 1) * 2048],
            )

        warm_ps = psum.tile([P, 512], F32, name="warm_ps", tag="s2", bufs=BANKS["s2"])
        for i in range(WARM):
            nc.tensor.matmul(warm_ps[:], zeros[:, 0:P], zeros[:], start=True, stop=True)
        at_tr(0)
        at_cp(0, True)
        ow_prep(0, True)
        ow_prep(1, False)
        at_q(0)
        ow_prep(2, False)
        ow_quant(0)
        ow_prep(3, False)
        s1_mm(0, 0, (0,))
        s1_mm(0, 1, (0,))
        at_tr(1)
        at_cp(1, False)
        ow_quant(1)
        s1_add(0, 0, (0,))
        s1_add(0, 1, (0,))
        s1_mm(0, 0, (1,))
        s1_mm(0, 1, (1,), "s2")
        s1_add(0, 0, (1,))
        sq(0, 0)
        at_q(1)
        s1_add(0, 1, (1,))
        at_tr(2)
        at_tr(3)
        nc.vector.tensor_copy(out=vperm[:].rearrange("p (t q i) -> p t q i", t=4, i=8), in_=vec[:].rearrange("p (q t i) -> p t q i", t=4, i=8))
        w_perm(0)
        w_perm(1)
        at_cp(2, False)
        s1_mm(1, 0)
        s1_mm(1, 1)
        at_cp(3, False)
        sq(0, 1)
        vps = psum.tile([P, 4, P], BF16, name="v_ps", tag="tp", bufs=BANKS["tp"])
        for t in range(4):
            nc.tensor.transpose(vps[:, t, :], vperm[:, t * P:(t + 1) * P], ident_b[:])
        s1_add(1, 0)
        w_tr(0, 0)
        w_tr(1, 0)
        s1_add(1, 1)
        sse(0, nc.gpsimd)
        rstd(0)
        at_q(2)
        at_q(3)
        w_perm(2)
        w_perm(3)
        s1_mm(2, 0)
        s1_mm(2, 1)
        sq(1, 0)
        nc.vector.tensor_copy(out=vcol[:], in_=vps[:, :, 0:6])
        s1_add(2, 0)
        sq(1, 1)
        s1_add(2, 1)
        w_tr(0, 1)
        w_tr(1, 1)
        nc.vector.scalar_tensor_tensor(out=g32[:], in0=vcol[:, :, 0:2], scalar=32.0, in1=vcol[:, :, 2:4], op0=ALU.mult, op1=ALU.mult)
        scale_y(0, 0, "vector")
        scale_y(0, 1, "vector")
        sse(1, nc.gpsimd)
        rstd(1)
        at_tr(4)
        sq(2, 0)
        w_quant(0)

        scale_y(1, 1, "vector", 1, 4)

        plan = []

        def add(step, slot, fn, *args):
            plan.append((step, slot, lambda: fn(*args)))

        FILL = 3
        for g in range(XB, NG):
            add(2 * (g - XB) + 3, 0, load_attn, g)
            add(2 * (g - XB) + 3, 0.5, load_x, g)
        for q in range(NQ):
            add(q - 1, 11, at_q, q)
            add(q - 2, 49, at_tr, q)
            add(q - 1, 3, at_cp, q, False)
            add(q, 30, s1_mm, q, 0)
            if q in (3, 4):
                add(q, 30.5, s1_mm, q, 1, (0, 1), "s2")
            else:
                add(q, 40, s1_mm, q, 1)
            add(q, 35, s1_add, q, 0)
            add(q, 45, s1_add, q, 1)
            add(q, 55, sq, q, 0)
            if q + 1 < NQ:
                add(q + 1, 4, sq, q, 1)
                add(q + 1, 14, sse, q)
                add(q + 1, 15, rstd, q)
                add(q + 1, 16, scale_y, q, 1, "gpsimd", 1, 4)
            if q + 2 < NQ:
                add(q + 2, 8, scale_y, q, 0, "vector")
                add(q + 2, 8.5, scale_y, q, 1, "vector", 0, 1)
        for g in range(NG - 1):
            a = 2 * g + 3
            for c8 in range(8):
                s = a + c8 // 4
                if s < NQ:
                    add(s, (31, 32, 33, 34)[c8 % 4], yt_tr, g, c8)
                    add(s, (34.1, 35, 36, 37)[c8 % 4], yt_aff, g, c8)
            for c in range(2):
                if a + 1 + c < NQ:
                    add(a + 1 + c, 10, regroup, g, c, 0, 512)
                    add(a + 1 + c, 12, hquant, g, c, 0, 512)
            for j in range(4):
                s, jj = a + 2 + j // 2 + j % 2, j % 2
                n = 4 * g + j
                if s < NQ:
                    add(s, (41, 29)[jj], s2_mm, n)
                    add(s, (57, 30)[jj], silu, n)
                if s + 1 - jj < NQ:
                    add(s + 1 - jj, (9.5, 38)[jj], ffmul, n)
        add(4, 9, w_quant, 1)
        for item in sorted((it for it in plan if it[0] >= FILL), key=lambda it: (it[0], it[1])):
            item[2]()

        g = NG - 1
        q = NQ - 1
        n = 4 * g
        scale_y(q - 1, 0, "vector")
        scale_y(q - 1, 1, "vector", 0, 1)
        ffmul(n - 8)
        s2_mm(n - 7)
        for c8 in range(4, 8):
            yt_tr(g - 1, c8, 0, 4, ("tp", "s1")[c8 // 7])
        for c8 in range(2):
            yt_tr(g, c8, 0, 2, "s1")
        sq(q, 1)
        silu(n - 7)
        regroup(g - 1, 0, 0, 512)
        for c8 in range(4, 8):
            yt_aff(g - 1, c8)
        sse(q)
        rstd(q)
        ffmul(n - 7)
        hquant(g - 1, 0, 0, 512)
        s2_mm(n - 6)
        for c8 in range(2, 5):
            yt_tr(g, c8, 0, 2, "tp")
        scale_y(q, 0, "vector")
        scale_y(q, 1, "vector")
        for c8 in range(2):
            yt_aff(g, c8, 0, 2)
        silu(n - 6)
        regroup(g - 1, 1, 0, 512)
        s2_mm(n - 5)
        for c8 in range(5, 8):
            yt_tr(g, c8, 0, 2, "s1")
        for c8 in range(2, 4):
            yt_aff(g, c8, 0, 2)
        ffmul(n - 6)
        hquant(g - 1, 1, 0, 512)
        silu(n - 5)
        for c8 in range(4, 6):
            yt_aff(g, c8, 0, 2)
        regroup(g, 0, 0, 256)
        for c8 in range(0, 3):
            yt_tr(g, c8, 2, 4, "tp")
        s2_mm(n - 4)
        for c8 in range(6, 8):
            yt_aff(g, c8, 0, 2)
        ffmul(n - 5)
        hquant(g, 0, 0, 256)
        yt_tr(g, 3, 2, 4, "s1")
        yt_tr(g, 4, 2, 4, "s1")
        silu(n - 4)
        s2_mm(n - 3)
        regroup(g, 1, 0, 256)
        for c8 in range(0, 4):
            yt_aff(g, c8, 2, 4, c8 == 3)
        ffmul(n - 4)
        hquant(g, 1, 0, 256)
        silu(n - 3)
        for c8 in range(5, 8):
            yt_tr(g, c8, 2, 4, "tp")
        for c8 in range(4, 8):
            yt_aff(g, c8, 2, 4)
        regroup(g, 0, 256, 512)
        s2_mm(n - 2)
        ffmul(n - 3)
        silu(n - 2)
        hquant(g, 0, 256, 512)
        regroup(g, 1, 256, 512)
        s2_mm(n - 1, "s1")
        s2_mm(n, "s1")
        s2_mm(n + 1, "s1")
        ffmul(n - 2)
        silu(n - 1)
        silu(n)
        silu(n + 1)
        hquant(g, 1, 256, 512)
        s2_mm(n + 2, "tp")
        s2_mm(n + 3, "tp")
        silu(n + 2)
        silu(n + 3)
        ffmul(n - 1)
        ffmul(n, 2)
        ffmul(n + 1, 2)
        ffmul(n + 2, 1)
        ffmul(n + 3, 1)
